import numpy as np
import ml_dtypes


def mxq(x, axis, fmt="e4m3"):
    dtype, down = {"e4m3": (ml_dtypes.float8_e4m3fn, 7), "e5m2": (ml_dtypes.float8_e5m2, 14)}[fmt]
    v = np.moveaxis(np.asarray(x, np.float32).astype(ml_dtypes.bfloat16).astype(np.float64), axis, -1)
    blocks = v.reshape(v.shape[:-1] + (-1, 32))
    amax = np.abs(blocks).max(-1, keepdims=True)
    byte = np.maximum(np.where(amax > 0, np.frexp(amax)[1] - 1 + 127, 0) - down, 1)
    scale = np.exp2(byte - 127.0)
    codes = (blocks / scale).astype(np.float32).astype(dtype).astype(np.float64)
    return np.moveaxis((codes * scale).reshape(v.shape), -1, axis)


WIDE = False


def mx_kscale(k):
    if not WIDE:
        return np.ones(k)
    levels = np.array([10, -10, 5, -5, 0])
    if k % 512:
        return np.exp2(np.random.permutation(np.resize(levels, k // 32))).repeat(32)
    a = np.empty((k // 512, 16))
    for p in range(k // 512):
        a[p, :8] = np.random.permutation(np.resize(levels, 8))
        for g in range(8):
            far = levels[np.abs(levels - a[p, g]) >= 10]
            a[p, g + 8] = far[np.random.randint(len(far))]
    return np.exp2(a.ravel()).repeat(32)


BF16 = ml_dtypes.bfloat16


def bf(x):
    return np.asarray(x, np.float32).astype(BF16)


def f64(x):
    return np.asarray(x).astype(np.float64)


B, V, H = 512, 128, 1024
G = 4 * H
EPS = 1e-5


def sigmoid(v):
    return 1.0 / (1.0 + np.exp(-v))


def layer_norm(v, w, b):
    mu = v.mean(-1, keepdims=True)
    var = ((v - mu) ** 2).mean(-1, keepdims=True)
    return (v - mu) / np.sqrt(var + EPS) * w + b


def setup_inputs():
    s = mx_kscale(H)
    return {"x": bf(np.random.standard_normal((B, V))),
            "h0": bf(np.random.standard_normal((B, H)) * s),
            "c0": bf(np.random.standard_normal((B, H))),
            "w_ih1": bf(np.random.standard_normal((G, V)) / np.sqrt(V)),
            "w_hh1": bf(np.random.standard_normal((G, H)) / np.sqrt(H) / s),
            "lni_w1": bf(1.0 + 0.1 * np.random.standard_normal(G)),
            "lni_b1": bf(0.1 * np.random.standard_normal(G)),
            "lnh_w1": bf(1.0 + 0.1 * np.random.standard_normal(G)),
            "lnh_b1": bf(0.1 * np.random.standard_normal(G)),
            "lnc_w1": bf(1.0 + 0.1 * np.random.standard_normal(H)),
            "lnc_b1": bf(0.1 * np.random.standard_normal(H))}


def reference(x, h0, c0, w_ih1, w_hh1, lni_w1, lni_b1, lnh_w1, lnh_b1, lnc_w1, lnc_b1):
    a = f64(x) @ f64(w_ih1).T
    r = mxq(f64(h0), 1, "e4m3") @ mxq(f64(w_hh1), 1, "e4m3").T
    gates = layer_norm(a, f64(lni_w1), f64(lni_b1)) + layer_norm(r, f64(lnh_w1), f64(lnh_b1))
    i, f, g, o = np.split(gates, 4, axis=1)
    cy = layer_norm(sigmoid(f) * f64(c0) + sigmoid(i) * np.tanh(g), f64(lnc_w1), f64(lnc_b1))
    hy = sigmoid(o) * np.tanh(cy)
    return hy, cy

@@ -1,0 +1,439 @@
+from contextlib import ExitStack
+
+import concourse.mybir as mybir
+from concourse.masks import make_identity
+
+F32 = mybir.dt.float32
+BF16 = mybir.dt.bfloat16
+U32 = mybir.dt.uint32
+U8 = mybir.dt.uint8
+FP8X4 = mybir.dt.float8_e4m3fn_x4
+ACT = mybir.ActivationFunctionType
+ALU = mybir.AluOpType
+
+P = 128
+B, V, H = 512, 128, 1024
+G = 4 * H
+EPS = 1e-5
+UNITS = B // P
+BANK = 512
+NB = G // BANK
+FLOPS = 2 * B * G * (H + V)
+PIN = True
+A_BANKS = 4
+POOL_UNITS = ()
+
+
+def tile_multilstm_pa_kernel(
+    tc, x, h0, c0, w_ih1, w_hh1, lni_w1, lni_b1, lnh_w1, lnh_b1, lnc_w1, lnc_b1, out_0, out_1
+):
+    nc = tc.nc
+    with ExitStack() as ctx:
+        if PIN:
+            ctx.enter_context(tc.manual_schedule())
+        const = ctx.enter_context(tc.tile_pool(name="const", bufs=1))
+        ld = ctx.enter_context(tc.tile_pool(name="ld", bufs=4))
+        grp_pool = ctx.enter_context(tc.tile_pool(name="grp", bufs=4))
+        big = ctx.enter_context(tc.tile_pool(name="big", bufs=6))
+        small = ctx.enter_context(tc.tile_pool(name="small", bufs=4))
+        ps_x = ctx.enter_context(tc.psum_pool(name="ps_x", bufs=4))
+        ps_a = ctx.enter_context(tc.psum_pool(name="ps_a", bufs=A_BANKS))
+
+        x_sb = const.tile([P, UNITS, V], BF16)
+        nc.sync.dma_start(out=x_sb[:], in_=x.rearrange("(u p) v -> p u v", p=P))
+        wih_sb = ld.tile([P, G // P, V], BF16, tag="ld")
+        for q in range(4):
+            nc.sync.dma_start(
+                out=wih_sb[:, 8 * q : 8 * q + 8, :],
+                in_=w_ih1[q * 1024 : (q + 1) * 1024, :].rearrange("(t p) v -> p t v", p=P),
+            )
+        wi_b = const.tile([P, G], BF16)
+        nc.sync.dma_start(out=wi_b[:], in_=lni_w1.partition_broadcast(P))
+        bi_b = ld.tile([P, G], BF16, tag="ld")
+        nc.sync.dma_start(out=bi_b[:], in_=lni_b1.partition_broadcast(P))
+        bh_b = ld.tile([P, G], BF16, tag="ld")
+        nc.sync.dma_start(out=bh_b[:], in_=lnh_b1.partition_broadcast(P))
+        h0_sb = ld.tile([P, UNITS, H], BF16, tag="ld")
+        nc.sync.dma_start(out=h0_sb[:], in_=h0.rearrange("(u p) k -> p u k", p=P))
+        whh_words = {}
+        for m in range(4):
+            wland = big.tile([P, 8, H], BF16, tag="big")
+            for hh in range(2):
+                n = 2 * m + hh
+                nc.sync.dma_start(
+                    out=wland[:, 4 * hh : 4 * hh + 4, :],
+                    in_=w_hh1[n * BANK : (n + 1) * BANK, :].rearrange("(t p) k -> p t k", p=P),
+                )
+                whh_words[n] = wland[:].bitcast(F32)[:, 4 * hh : 4 * hh + 4, :]
+
+        ident_b = const.tile([P, P], BF16)
+        make_identity(nc, ident_b[:])
+        ident_f = const.tile([P, P], F32)
+        make_identity(nc, ident_f[:])
+        neghalf = const.tile([P, UNITS], F32)
+        nc.vector.memset(neghalf[:], -0.5)
+
+        xT = const.tile([P, B], BF16)
+        xT_f = const.tile([P, B], F32)
+        gram = const.tile([P, V + 4], F32)
+        tpx = ps_x.tile([P, UNITS, P], BF16, tag="x")
+        for u in range(UNITS):
+            nc.tensor.transpose(tpx[:, u, :], x_sb[:, u, :], ident_b[:])
+        nc.scalar.copy(out=xT[:], in_=tpx[:].rearrange("p u b -> p (u b)"))
+        nc.scalar.copy(out=xT_f[:], in_=tpx[:].rearrange("p u b -> p (u b)"))
+        wihT = const.tile([P, G], BF16)
+        gram_ps = ps_a.tile([P, V], F32, tag="mma")
+        for q in range(4):
+            tpw = ps_x.tile([P, 8, P], BF16, tag="x")
+            for j in range(8):
+                nc.tensor.transpose(tpw[:, j, :], wih_sb[:, 8 * q + j, :], ident_b[:])
+            nc.scalar.activation(
+                out=wihT[:, q * 1024 : (q + 1) * 1024],
+                in_=tpw[:].rearrange("p j g -> p (j g)"),
+                func=ACT.Identity,
+                accum_out=gram[:, V + q : V + q + 1],
+            )
+            for j in range(8):
+                t = 8 * q + j
+                nc.tensor.matmul(
+                    out=gram_ps[:], lhsT=wih_sb[:, t, :], rhs=wih_sb[:, t, :], start=(t == 0), stop=(t == G // P - 1)
+                )
+        nc.scalar.copy(out=gram[:, 0:V], in_=gram_ps[:])
+
+        bs = const.tile([P, G], F32)
+
+        def bias_sum(k):
+            cols = slice(k * H, (k + 1) * H)
+            nc.gpsimd.tensor_tensor(out=bs[:, cols], in0=bi_b[:, cols], in1=bh_b[:, cols], op=ALU.add)
+
+        bias_sum(0)
+
+        q4 = small.tile([P, UNITS], F32, tag="q4")
+        mean4 = small.tile([P, UNITS], F32, tag="mean4")
+        for u in range(UNITS):
+            y_ps = ps_a.tile([P, V + 4], F32, tag="mma")
+            nc.tensor.matmul(out=y_ps[:], lhsT=xT_f[:, u * P : (u + 1) * P], rhs=gram[:], start=True, stop=True)
+            yjunk = small.tile([P, V], F32, tag="yjunk")
+            nc.vector.scalar_tensor_tensor(
+                out=yjunk[:], in0=y_ps[:, 0:V], scalar=1.0 / G, in1=x_sb[:, u, :], op0=ALU.mult, op1=ALU.mult,
+                accum_out=q4[:, u : u + 1],
+            )
+            mjunk = small.tile([P, 4], F32, tag="mjunk")
+            nc.vector.tensor_scalar(
+                out=mjunk[:], in0=y_ps[:, V : V + 4], scalar1=1.0 / G, scalar2=None, op0=ALU.mult, op1=ALU.add,
+                accum_out=mean4[:, u : u + 1],
+            )
+        msq4 = small.tile([P, UNITS], F32, tag="msq4")
+        nc.vector.tensor_tensor(out=msq4[:], in0=mean4[:], in1=mean4[:], op=ALU.mult)
+        var4 = small.tile([P, UNITS], F32, tag="var4")
+        nc.vector.tensor_tensor(out=var4[:], in0=q4[:], in1=msq4[:], op=ALU.subtract)
+        veps4 = small.tile([P, UNITS], F32, tag="veps4")
+        nc.gpsimd.tensor_scalar(out=veps4[:], in0=var4[:], scalar1=0.0, scalar2=EPS, op0=ALU.max, op1=ALU.add)
+        rstd4 = small.tile([P, UNITS], F32, tag="rstd4")
+        nc.gpsimd.tensor_tensor(out=rstd4[:], in0=veps4[:], in1=neghalf[:], op=ALU.pow)
+        for k in range(1, 4):
+            bias_sum(k)
+
+        wh_b = ld.tile([P, G], BF16, tag="ld")
+        nc.sync.dma_start(out=wh_b[:], in_=lnh_w1.partition_broadcast(P))
+        lwlb = ld.tile([P, 2, H], BF16, tag="ld")
+        nc.sync.dma_start(out=lwlb[:, 0, :], in_=lnc_w1.partition_broadcast(P))
+        nc.sync.dma_start(out=lwlb[:, 1, :], in_=lnc_b1.partition_broadcast(P))
+
+        h_codes = const.tile([P, 2, B], U32, align_bytes=64)
+        h_scales = const.tile([P, 2, B], U8, align_bytes=64)
+        w_codes = const.tile([P, 2, G], U32, align_bytes=64)
+        w_scales = const.tile([P, 2, G], U8, align_bytes=64)
+        grp_tiles = {}
+
+        def transpose_rows(key, src_words):
+            for c in range(2):
+                grp = grp_pool.tile([P, 4 * BANK], BF16, tag="grp", align_bytes=64)
+                grpw = grp[:].bitcast(F32).rearrange("p (r s) -> p r s", s=2)
+                for half in range(2):
+                    tp = ps_x.tile([P, 2, 256], F32, tag="x")
+                    for s in range(2):
+                        for j in range(2):
+                            nc.tensor.transpose(
+                                tp[:, s, j * P : (j + 1) * P],
+                                src_words[:, 2 * half + j, 256 * c + s : 256 * (c + 1) : 2],
+                                ident_f[:],
+                            )
+                    nc.scalar.copy(
+                        out=grpw[:, half * 256 : (half + 1) * 256, :], in_=tp[:].rearrange("p s r -> p r s")
+                    )
+                grp_tiles[(key, c)] = grp
+
+        def quantise(key, codes, scales):
+            for c in range(2):
+                nc.vector.quantize_mx(
+                    out=codes[:, c, :].bitcast(FP8X4), scales=scales[:, c, :], in_=grp_tiles[(key, c)][:]
+                )
+
+        def prep_whh(n):
+            transpose_rows(n, whh_words[n])
+
+        def quantise_whh(n):
+            cols = slice(n * BANK, (n + 1) * BANK)
+            quantise(n, w_codes[:, :, cols], w_scales[:, :, cols])
+
+        a_tiles = {}
+        a_banks = {}
+
+        def a_matmul(k):
+            if k >= UNITS * NB:
+                return
+            u, n = divmod(k, NB)
+            acc = ps_a.tile([P, BANK], F32, tag="mma")
+            nc.tensor.matmul(
+                out=acc[:], lhsT=xT[:, u * P : (u + 1) * P], rhs=wihT[:, n * BANK : (n + 1) * BANK],
+                start=True, stop=True,
+            )
+            a_banks[k] = acc
+
+        def t1(k):
+            u, n = divmod(k, NB)
+            if n == 0:
+                a_new = big.tile([P, G], F32, tag="big")
+                a_tiles[u] = a_new
+            cols = slice(n * BANK, (n + 1) * BANK)
+            nc.vector.scalar_tensor_tensor(
+                out=a_tiles[u][:, cols], in0=a_banks[k][:], scalar=mean4[:, u : u + 1], in1=wi_b[:, cols],
+                op0=ALU.subtract, op1=ALU.mult,
+            )
+
+        def t1_group(g):
+            for k in range(4 * g, 4 * g + 4):
+                t1(k)
+                a_matmul(k + A_BANKS)
+
+        def c1(g):
+            u, half = divmod(g, 2)
+            cols = slice(half * 2048, (half + 1) * 2048)
+            nc.vector.scalar_tensor_tensor(
+                out=a_tiles[u][:, cols], in0=a_tiles[u][:, cols], scalar=rstd4[:, u : u + 1], in1=bs[:, cols],
+                op0=ALU.mult, op1=ALU.add,
+            )
+
+        r_tiles = {}
+        st = {}
+
+        def r_evict(u, banks):
+            rows = slice(u * P, (u + 1) * P)
+            if u not in r_tiles:
+                r_new = big.tile([P, G], F32, tag="big")
+                r_tiles[u] = r_new
+                s1 = small.tile([P, NB], F32, tag="s1")
+                st[("s1", u)] = s1
+            for n in banks:
+                cols = slice(n * BANK, (n + 1) * BANK)
+                acc = ps_x.tile([P, BANK], F32, tag="x")
+                for c in range(2):
+                    nc.tensor.matmul_mx(
+                        out=acc[:],
+                        lhsT=h_codes[:, c, rows].bitcast(FP8X4),
+                        lhsT_scale=h_scales[:, c, rows],
+                        rhs=w_codes[:, c, cols].bitcast(FP8X4),
+                        rhs_scale=w_scales[:, c, cols],
+                        start=(c == 0),
+                        stop=(c == 1),
+                    )
+                nc.scalar.activation(
+                    out=r_tiles[u][:, cols], in_=acc[:], func=ACT.Identity, accum_out=st[("s1", u)][:, n : n + 1]
+                )
+
+        def r_mean(u):
+            s1junk = small.tile([P, NB], F32, tag="s1junk")
+            negmean = small.tile([P, 1], F32, tag="negmean")
+            nc.scalar.activation(
+                out=s1junk[:], in_=st[("s1", u)][:], func=ACT.Identity, scale=-1.0 / G, accum_out=negmean[:]
+            )
+            ssq = small.tile([P, 2], F32, tag="ssq")
+            st[("negmean", u)] = negmean
+            st[("ssq", u)] = ssq
+
+        def r_var(u, k):
+            junk = grp_pool.tile([P, 2048], BF16, tag="grp", align_bytes=64)
+            nc.scalar.activation(
+                out=junk[:], in_=r_tiles[u][:, k * 2048 : (k + 1) * 2048], func=ACT.Square,
+                bias=st[("negmean", u)][:, 0:1], scale=1.0, accum_out=st[("ssq", u)][:, k : k + 1],
+            )
+            if k == 1:
+                ssq = st[("ssq", u)]
+                vjunk = small.tile([P, 2], F32, tag="vjunk")
+                veps = small.tile([P, 1], F32, tag="veps")
+                nc.scalar.activation(
+                    out=vjunk[:], in_=ssq[:], func=ACT.Identity, bias=EPS / 2.0, scale=1.0 / G, accum_out=veps[:]
+                )
+                rstd = small.tile([P, 1], F32, tag="rstd")
+                nc.gpsimd.tensor_tensor(out=rstd[:], in0=veps[:], in1=neghalf[:, 0:1], op=ALU.pow)
+                st[("rstd", u)] = rstd
+
+        def t2(u, k):
+            cols = slice(k * H, (k + 1) * H)
+            nc.vector.scalar_tensor_tensor(
+                out=r_tiles[u][:, cols], in0=r_tiles[u][:, cols], scalar=st[("negmean", u)][:, 0:1],
+                in1=wh_b[:, cols], op0=ALU.add, op1=ALU.mult,
+            )
+
+        funcs = [ACT.Sigmoid, ACT.Sigmoid, ACT.Tanh, ACT.Sigmoid]
+
+        def c2(u, k):
+            cols = slice(k * H, (k + 1) * H)
+            nc.vector.scalar_tensor_tensor(
+                out=r_tiles[u][:, cols], in0=r_tiles[u][:, cols], scalar=st[("rstd", u)][:, 0:1],
+                in1=a_tiles[u][:, cols], op0=ALU.mult, op1=ALU.add,
+            )
+            nc.scalar.activation(out=r_tiles[u][:, cols], in_=r_tiles[u][:, cols], func=funcs[k])
+
+        def gate(u, k):
+            return r_tiles[u][:, k * H : (k + 1) * H]
+
+        def side(u):
+            return nc.gpsimd if u in POOL_UNITS else nc.vector
+
+        def m1(u):
+            side(u).tensor_tensor(out=gate(u, 1), in0=gate(u, 1), in1=c0_sb[:, u, :], op=ALU.mult)
+
+        def m2_cp(u):
+            nc.vector.tensor_tensor(out=gate(u, 0), in0=gate(u, 0), in1=gate(u, 2), op=ALU.mult)
+            csum = small.tile([P, 1], F32, tag="csum")
+            nc.vector.scalar_tensor_tensor(
+                out=gate(u, 0), in0=gate(u, 0), scalar=1.0, in1=gate(u, 1), op0=ALU.mult, op1=ALU.add,
+                accum_out=csum[:],
+            )
+            cneg = small.tile([P, 1], F32, tag="cneg")
+            nc.vector.tensor_scalar(out=cneg[:], in0=csum[:], scalar1=-1.0 / H, scalar2=None, op0=ALU.mult)
+            st[("cneg", u)] = cneg
+
+        def c_var(u):
+            cssq = small.tile([P, 1], F32, tag="cssq")
+            cjunk = grp_pool.tile([P, 2048], BF16, tag="grp", align_bytes=64)
+            nc.scalar.activation(
+                out=cjunk[:, 0:H], in_=gate(u, 0), func=ACT.Square, bias=st[("cneg", u)][:, 0:1], scale=1.0,
+                accum_out=cssq[:],
+            )
+            cveps = small.tile([P, 1], F32, tag="cveps")
+            nc.scalar.activation(out=cveps[:], in_=cssq[:], func=ACT.Identity, bias=EPS, scale=1.0 / H)
+            crstd = small.tile([P, 1], F32, tag="crstd")
+            nc.gpsimd.tensor_tensor(out=crstd[:], in0=cveps[:], in1=neghalf[:, 0:1], op=ALU.pow)
+            st[("crstd", u)] = crstd
+
+        def cy1(u):
+            nc.vector.scalar_tensor_tensor(
+                out=gate(u, 2), in0=gate(u, 0), scalar=st[("cneg", u)][:, 0:1], in1=lwlb[:, 0, :],
+                op0=ALU.add, op1=ALU.mult,
+            )
+
+        def cy(u):
+            nc.vector.scalar_tensor_tensor(
+                out=gate(u, 1), in0=gate(u, 2), scalar=st[("crstd", u)][:, 0:1], in1=lwlb[:, 1, :],
+                op0=ALU.mult, op1=ALU.add,
+            )
+            nc.sync.dma_start(out=out_1[u * P : (u + 1) * P, :], in_=gate(u, 1))
+
+        def half(u, k, hh):
+            return r_tiles[u][:, k * H + hh * BANK : k * H + (hh + 1) * BANK]
+
+        def cy_half(u, hh):
+            cols = slice(hh * BANK, (hh + 1) * BANK)
+            nc.vector.scalar_tensor_tensor(
+                out=half(u, 1, hh), in0=half(u, 2, hh), scalar=st[("crstd", u)][:, 0:1], in1=lwlb[:, 1, cols],
+                op0=ALU.mult, op1=ALU.add,
+            )
+            nc.sync.dma_start(out=out_1[u * P : (u + 1) * P, cols], in_=half(u, 1, hh))
+            nc.scalar.activation(out=half(u, 0, hh), in_=half(u, 1, hh), func=ACT.Tanh)
+
+        def hy_half(u, hh):
+            cols = slice(hh * BANK, (hh + 1) * BANK)
+            nc.vector.tensor_tensor(out=half(u, 3, hh), in0=half(u, 3, hh), in1=half(u, 0, hh), op=ALU.mult)
+            nc.sync.dma_start(out=out_0[u * P : (u + 1) * P, cols], in_=half(u, 3, hh))
+
+        def c_tanh(u):
+            nc.scalar.activation(out=gate(u, 0), in_=gate(u, 1), func=ACT.Tanh)
+
+        def hy(u):
+            side(u).tensor_tensor(out=gate(u, 3), in0=gate(u, 3), in1=gate(u, 0), op=ALU.mult)
+            nc.sync.dma_start(out=out_0[u * P : (u + 1) * P, :], in_=gate(u, 3))
+
+        for k in range(A_BANKS):
+            a_matmul(k)
+        t1_group(0)
+        transpose_rows("h", h0_sb[:].bitcast(F32))
+        c0_sb = ld.tile([P, UNITS, H], BF16, tag="ld")
+        nc.sync.dma_start(out=c0_sb[:], in_=c0.rearrange("(u p) k -> p u k", p=P))
+        prep_whh(0)
+        t1_group(1)
+        quantise("h", h_codes, h_scales)
+        prep_whh(1)
+        c1(0)
+        quantise_whh(0)
+        prep_whh(2)
+        c1(1)
+        for g in range(2, 5):
+            quantise_whh(2 * g - 3)
+            prep_whh(2 * g - 1)
+            t1_group(g)
+            quantise_whh(2 * g - 2)
+            if 2 * g < NB:
+                prep_whh(2 * g)
+            c1(g)
+        quantise_whh(7)
+        r_evict(0, range(NB))
+        r_mean(0)
+        t1_group(5)
+        c1(5)
+        t1_group(6)
+        r_var(0, 0)
+        r_var(0, 1)
+        r_evict(1, range(NB))
+        r_mean(1)
+        c1(6)
+        t1_group(7)
+        r_var(1, 0)
+        r_var(1, 1)
+        c1(7)
+
+        for k in range(4):
+            t2(0, k)
+        for u in range(UNITS - 1):
+            far = u + 2 < UNITS
+            c2(u, 1)
+            c2(u, 0)
+            c2(u, 2)
+            c2(u, 3)
+            if u > 0:
+                hy(u - 1)
+            if far:
+                r_evict(u + 2, range(0, 6))
+            t2(u + 1, 0)
+            t2(u + 1, 1)
+            m1(u)
+            m2_cp(u)
+            c_var(u)
+            if far:
+                r_evict(u + 2, range(6, NB))
+                r_mean(u + 2)
+            t2(u + 1, 2)
+            cy1(u)
+            t2(u + 1, 3)
+            if far:
+                r_var(u + 2, 0)
+            cy(u)
+            c_tanh(u)
+            if far:
+                r_var(u + 2, 1)
+        last = UNITS - 1
+        c2(last, 1)
+        c2(last, 0)
+        c2(last, 2)
+        c2(last, 3)
+        m1(last)
+        m2_cp(last)
+        c_var(last)
+        cy1(last)
+        hy(last - 1)
+        cy_half(last, 0)
+        cy_half(last, 1)
+        hy_half(last, 0)
+        hy_half(last, 1)

@@ -18,10 +18,9 @@ EPS = 1e-5
 UNITS = B // P
 BANK = 512
 NB = G // BANK
+GT = G // P
+VW = 144
 FLOPS = 2 * B * G * (H + V)
-PIN = True
-A_BANKS = 4
-POOL_UNITS = ()
 
 
 def tile_multilstm_pa_kernel(
@@ -29,34 +28,34 @@ def tile_multilstm_pa_kernel(
 ):
     nc = tc.nc
     with ExitStack() as ctx:
-        if PIN:
-            ctx.enter_context(tc.manual_schedule())
+        ctx.enter_context(tc.manual_schedule())
         const = ctx.enter_context(tc.tile_pool(name="const", bufs=1))
-        ld = ctx.enter_context(tc.tile_pool(name="ld", bufs=4))
-        grp_pool = ctx.enter_context(tc.tile_pool(name="grp", bufs=4))
-        big = ctx.enter_context(tc.tile_pool(name="big", bufs=6))
+        grp_pool = ctx.enter_context(tc.tile_pool(name="grp", bufs=6))
+        big = ctx.enter_context(tc.tile_pool(name="big", bufs=5))
         small = ctx.enter_context(tc.tile_pool(name="small", bufs=4))
-        ps_x = ctx.enter_context(tc.psum_pool(name="ps_x", bufs=4))
-        ps_a = ctx.enter_context(tc.psum_pool(name="ps_a", bufs=A_BANKS))
+        ps = ctx.enter_context(tc.psum_pool(name="ps", bufs=4))
+
+        wih_sb = const.tile([P, GT, VW], BF16)
+        nc.gpsimd.memset(wih_sb[:, :, V:VW], 1.0)
+        brow = const.tile([P, P], BF16)
+        nc.vector.memset(brow[64:128, :], 0.0)
+        neghalf = const.tile([P, UNITS], F32)
+        nc.vector.memset(neghalf[:], -0.5)
 
         x_sb = const.tile([P, UNITS, V], BF16)
         nc.sync.dma_start(out=x_sb[:], in_=x.rearrange("(u p) v -> p u v", p=P))
-        wih_sb = ld.tile([P, G // P, V], BF16, tag="ld")
         for q in range(4):
             nc.sync.dma_start(
-                out=wih_sb[:, 8 * q : 8 * q + 8, :],
+                out=wih_sb[:, 8 * q : 8 * q + 8, 0:V],
                 in_=w_ih1[q * 1024 : (q + 1) * 1024, :].rearrange("(t p) v -> p t v", p=P),
             )
         wi_b = const.tile([P, G], BF16)
         nc.sync.dma_start(out=wi_b[:], in_=lni_w1.partition_broadcast(P))
-        bi_b = ld.tile([P, G], BF16, tag="ld")
-        nc.sync.dma_start(out=bi_b[:], in_=lni_b1.partition_broadcast(P))
-        bh_b = ld.tile([P, G], BF16, tag="ld")
-        nc.sync.dma_start(out=bh_b[:], in_=lnh_b1.partition_broadcast(P))
-        h0_sb = ld.tile([P, UNITS, H], BF16, tag="ld")
+        h0_sb = const.tile([P, UNITS, H], BF16)
         nc.sync.dma_start(out=h0_sb[:], in_=h0.rearrange("(u p) k -> p u k", p=P))
         whh_words = {}
-        for m in range(4):
+
+        def load_whh(m):
             wland = big.tile([P, 8, H], BF16, tag="big")
             for hh in range(2):
                 n = 2 * m + hh
@@ -66,92 +65,91 @@ def tile_multilstm_pa_kernel(
                 )
                 whh_words[n] = wland[:].bitcast(F32)[:, 4 * hh : 4 * hh + 4, :]
 
+        load_whh(0)
+        nc.sync.dma_start(out=brow[0:32, :], in_=lni_b1.rearrange("(t p) -> t p", p=P))
+        nc.sync.dma_start(out=brow[32:64, :], in_=lnh_b1.rearrange("(t p) -> t p", p=P))
+        load_whh(1)
+        load_whh(2)
+        wh_b = const.tile([P, G], BF16)
+        r_tiles = {}
+        st = {}
+
+        def r_open(u):
+            r_new = big.tile([P, G], F32, tag="big")
+            r_tiles[u] = r_new
+            s1 = small.tile([P, NB], F32, tag="s1")
+            st[("s1", u)] = s1
+
+        r_open(0)
+        r_open(1)
+        c0_sb = const.tile([P, UNITS, H], BF16)
+        lwlb = const.tile([P, 2, H], BF16)
+
+        def load_rest():
+            load_whh(3)
+            nc.sync.dma_start(out=wh_b[:], in_=lnh_w1.partition_broadcast(P))
+            nc.sync.dma_start(out=c0_sb[:], in_=c0.rearrange("(u p) k -> p u k", p=P))
+            nc.sync.dma_start(out=lwlb[:, 0, :], in_=lnc_w1.partition_broadcast(P))
+            nc.sync.dma_start(out=lwlb[:, 1, :], in_=lnc_b1.partition_broadcast(P))
+
         ident_b = const.tile([P, P], BF16)
         make_identity(nc, ident_b[:])
         ident_f = const.tile([P, P], F32)
         make_identity(nc, ident_f[:])
-        neghalf = const.tile([P, UNITS], F32)
-        nc.vector.memset(neghalf[:], -0.5)
 
-        xT = const.tile([P, B], BF16)
         xT_f = const.tile([P, B], F32)
-        gram = const.tile([P, V + 4], F32)
-        tpx = ps_x.tile([P, UNITS, P], BF16, tag="x")
+        tpx = ps.tile([P, UNITS, P], BF16, tag="r", bufs=3)
         for u in range(UNITS):
             nc.tensor.transpose(tpx[:, u, :], x_sb[:, u, :], ident_b[:])
-        nc.scalar.copy(out=xT[:], in_=tpx[:].rearrange("p u b -> p (u b)"))
         nc.scalar.copy(out=xT_f[:], in_=tpx[:].rearrange("p u b -> p (u b)"))
-        wihT = const.tile([P, G], BF16)
-        gram_ps = ps_a.tile([P, V], F32, tag="mma")
-        for q in range(4):
-            tpw = ps_x.tile([P, 8, P], BF16, tag="x")
-            for j in range(8):
-                nc.tensor.transpose(tpw[:, j, :], wih_sb[:, 8 * q + j, :], ident_b[:])
-            nc.scalar.activation(
-                out=wihT[:, q * 1024 : (q + 1) * 1024],
-                in_=tpw[:].rearrange("p j g -> p (j g)"),
-                func=ACT.Identity,
-                accum_out=gram[:, V + q : V + q + 1],
+        gram_ps = ps.tile([P, V + 1], F32, tag="r", bufs=3)
+        for t in range(GT):
+            nc.tensor.matmul(
+                out=gram_ps[:], lhsT=wih_sb[:, t, 0:V], rhs=wih_sb[:, t, 0 : V + 1], start=(t == 0), stop=(t == GT - 1)
             )
-            for j in range(8):
-                t = 8 * q + j
-                nc.tensor.matmul(
-                    out=gram_ps[:], lhsT=wih_sb[:, t, :], rhs=wih_sb[:, t, :], start=(t == 0), stop=(t == G // P - 1)
-                )
-        nc.scalar.copy(out=gram[:, 0:V], in_=gram_ps[:])
+        gram = const.tile([P, V + 1], F32)
+        nc.scalar.copy(out=gram[:], in_=gram_ps[:])
+        wneg = const.tile([P, 1], F32)
+        nc.scalar.activation(out=wneg[:], in_=gram[:, V : V + 1], func=ACT.Identity, scale=-1.0 / G)
 
-        bs = const.tile([P, G], F32)
-
-        def bias_sum(k):
-            cols = slice(k * H, (k + 1) * H)
-            nc.gpsimd.tensor_tensor(out=bs[:, cols], in0=bi_b[:, cols], in1=bh_b[:, cols], op=ALU.add)
-
-        bias_sum(0)
-
-        q4 = small.tile([P, UNITS], F32, tag="q4")
-        mean4 = small.tile([P, UNITS], F32, tag="mean4")
+        q4 = const.tile([P, UNITS], F32)
+        mean4 = const.tile([P, UNITS], F32)
         for u in range(UNITS):
-            y_ps = ps_a.tile([P, V + 4], F32, tag="mma")
+            y_ps = ps.tile([P, V + 1], F32, tag="r", bufs=3)
             nc.tensor.matmul(out=y_ps[:], lhsT=xT_f[:, u * P : (u + 1) * P], rhs=gram[:], start=True, stop=True)
             yjunk = small.tile([P, V], F32, tag="yjunk")
             nc.vector.scalar_tensor_tensor(
                 out=yjunk[:], in0=y_ps[:, 0:V], scalar=1.0 / G, in1=x_sb[:, u, :], op0=ALU.mult, op1=ALU.mult,
                 accum_out=q4[:, u : u + 1],
             )
-            mjunk = small.tile([P, 4], F32, tag="mjunk")
             nc.vector.tensor_scalar(
-                out=mjunk[:], in0=y_ps[:, V : V + 4], scalar1=1.0 / G, scalar2=None, op0=ALU.mult, op1=ALU.add,
-                accum_out=mean4[:, u : u + 1],
+                out=mean4[:, u : u + 1], in0=y_ps[:, V : V + 1], scalar1=1.0 / G, scalar2=None, op0=ALU.mult
             )
-        msq4 = small.tile([P, UNITS], F32, tag="msq4")
+        msq4 = const.tile([P, UNITS], F32)
         nc.vector.tensor_tensor(out=msq4[:], in0=mean4[:], in1=mean4[:], op=ALU.mult)
-        var4 = small.tile([P, UNITS], F32, tag="var4")
+        var4 = const.tile([P, UNITS], F32)
         nc.vector.tensor_tensor(out=var4[:], in0=q4[:], in1=msq4[:], op=ALU.subtract)
-        veps4 = small.tile([P, UNITS], F32, tag="veps4")
+        veps4 = const.tile([P, UNITS], F32)
         nc.gpsimd.tensor_scalar(out=veps4[:], in0=var4[:], scalar1=0.0, scalar2=EPS, op0=ALU.max, op1=ALU.add)
-        rstd4 = small.tile([P, UNITS], F32, tag="rstd4")
+        rstd4 = const.tile([P, UNITS], F32)
         nc.gpsimd.tensor_tensor(out=rstd4[:], in0=veps4[:], in1=neghalf[:], op=ALU.pow)
-        for k in range(1, 4):
-            bias_sum(k)
-
-        wh_b = ld.tile([P, G], BF16, tag="ld")
-        nc.sync.dma_start(out=wh_b[:], in_=lnh_w1.partition_broadcast(P))
-        lwlb = ld.tile([P, 2, H], BF16, tag="ld")
-        nc.sync.dma_start(out=lwlb[:, 0, :], in_=lnc_w1.partition_broadcast(P))
-        nc.sync.dma_start(out=lwlb[:, 1, :], in_=lnc_b1.partition_broadcast(P))
 
         h_codes = const.tile([P, 2, B], U32, align_bytes=64)
         h_scales = const.tile([P, 2, B], U8, align_bytes=64)
         w_codes = const.tile([P, 2, G], U32, align_bytes=64)
         w_scales = const.tile([P, 2, G], U8, align_bytes=64)
+        wT = const.tile([P, G], F32)
+        xs = const.tile([P, UNITS, V], F32)
+        xsT = const.tile([P, B], F32)
+        bcol = const.tile([P, GT], F32)
         grp_tiles = {}
 
-        def transpose_rows(key, src_words):
+        def transpose_rows(key, src_words, on_vector):
             for c in range(2):
                 grp = grp_pool.tile([P, 4 * BANK], BF16, tag="grp", align_bytes=64)
                 grpw = grp[:].bitcast(F32).rearrange("p (r s) -> p r s", s=2)
                 for half in range(2):
-                    tp = ps_x.tile([P, 2, 256], F32, tag="x")
+                    tp = ps.tile([P, 2, 256], F32, tag="x", bufs=5)
                     for s in range(2):
                         for j in range(2):
                             nc.tensor.transpose(
@@ -159,9 +157,12 @@ def tile_multilstm_pa_kernel(
                                 src_words[:, 2 * half + j, 256 * c + s : 256 * (c + 1) : 2],
                                 ident_f[:],
                             )
-                    nc.scalar.copy(
-                        out=grpw[:, half * 256 : (half + 1) * 256, :], in_=tp[:].rearrange("p s r -> p r s")
-                    )
+                    dst = grpw[:, half * 256 : (half + 1) * 256, :]
+                    src = tp[:].rearrange("p s r -> p r s")
+                    if 2 * c + half in on_vector:
+                        nc.vector.tensor_copy(out=dst, in_=src)
+                    else:
+                        nc.scalar.copy(out=dst, in_=src)
                 grp_tiles[(key, c)] = grp
 
         def quantise(key, codes, scales):
@@ -170,77 +171,82 @@ def tile_multilstm_pa_kernel(
                     out=codes[:, c, :].bitcast(FP8X4), scales=scales[:, c, :], in_=grp_tiles[(key, c)][:]
                 )
 
-        def prep_whh(n):
-            transpose_rows(n, whh_words[n])
-
         def quantise_whh(n):
             cols = slice(n * BANK, (n + 1) * BANK)
             quantise(n, w_codes[:, :, cols], w_scales[:, :, cols])
 
-        a_tiles = {}
+        def prep_wT(q):
+            tpw = ps.tile([P, 8, P], BF16, tag="r", bufs=3)
+            for j in range(8):
+                nc.tensor.transpose(tpw[:, j, :], wih_sb[:, 8 * q + j, 0:V], ident_b[:])
+            cols = slice(q * 1024, (q + 1) * 1024)
+            nc.vector.scalar_tensor_tensor(
+                out=wT[:, cols], in0=tpw[:].rearrange("p j g -> p (j g)"), scalar=wneg[:, 0:1], in1=wi_b[:, cols],
+                op0=ALU.add, op1=ALU.mult,
+            )
+
+        def prep_bias():
+            tpb = ps.tile([P, P], BF16, tag="r", bufs=3)
+            nc.tensor.transpose(tpb[:], brow[:], ident_b[:])
+            b2 = const.tile([P, 64], F32)
+            nc.scalar.copy(out=b2[:], in_=tpb[:, 0:64])
+            nc.vector.tensor_tensor(out=bcol[:], in0=b2[:, 0:GT], in1=b2[:, GT : 2 * GT], op=ALU.add)
+
+        def prep_xs():
+            for u in range(UNITS):
+                nc.vector.tensor_scalar(
+                    out=xs[:, u, :], in0=x_sb[:, u, :], scalar1=rstd4[:, u : u + 1], scalar2=None, op0=ALU.mult
+                )
+            tps = ps.tile([P, UNITS, P], F32, tag="r", bufs=3)
+            for u in range(UNITS):
+                nc.tensor.transpose(tps[:, u, :], xs[:, u, :], ident_f[:])
+            nc.scalar.copy(out=xsT[:], in_=tps[:].rearrange("p u b -> p (u b)"))
+
         a_banks = {}
 
-        def a_matmul(k):
-            if k >= UNITS * NB:
-                return
-            u, n = divmod(k, NB)
-            acc = ps_a.tile([P, BANK], F32, tag="mma")
-            nc.tensor.matmul(
-                out=acc[:], lhsT=xT[:, u * P : (u + 1) * P], rhs=wihT[:, n * BANK : (n + 1) * BANK],
-                start=True, stop=True,
-            )
-            a_banks[k] = acc
-
-        def t1(k):
-            u, n = divmod(k, NB)
-            if n == 0:
-                a_new = big.tile([P, G], F32, tag="big")
-                a_tiles[u] = a_new
-            cols = slice(n * BANK, (n + 1) * BANK)
-            nc.vector.scalar_tensor_tensor(
-                out=a_tiles[u][:, cols], in0=a_banks[k][:], scalar=mean4[:, u : u + 1], in1=wi_b[:, cols],
-                op0=ALU.subtract, op1=ALU.mult,
-            )
-
-        def t1_group(g):
-            for k in range(4 * g, 4 * g + 4):
-                t1(k)
-                a_matmul(k + A_BANKS)
-
-        def c1(g):
-            u, half = divmod(g, 2)
-            cols = slice(half * 2048, (half + 1) * 2048)
-            nc.vector.scalar_tensor_tensor(
-                out=a_tiles[u][:, cols], in0=a_tiles[u][:, cols], scalar=rstd4[:, u : u + 1], in1=bs[:, cols],
-                op0=ALU.mult, op1=ALU.add,
-            )
-
-        r_tiles = {}
-        st = {}
-
-        def r_evict(u, banks):
-            rows = slice(u * P, (u + 1) * P)
-            if u not in r_tiles:
-                r_new = big.tile([P, G], F32, tag="big")
-                r_tiles[u] = r_new
-                s1 = small.tile([P, NB], F32, tag="s1")
-                st[("s1", u)] = s1
-            for n in banks:
-                cols = slice(n * BANK, (n + 1) * BANK)
-                acc = ps_x.tile([P, BANK], F32, tag="x")
-                for c in range(2):
-                    nc.tensor.matmul_mx(
-                        out=acc[:],
-                        lhsT=h_codes[:, c, rows].bitcast(FP8X4),
-                        lhsT_scale=h_scales[:, c, rows],
-                        rhs=w_codes[:, c, cols].bitcast(FP8X4),
-                        rhs_scale=w_scales[:, c, cols],
-                        start=(c == 0),
-                        stop=(c == 1),
-                    )
-                nc.scalar.activation(
-                    out=r_tiles[u][:, cols], in_=acc[:], func=ACT.Identity, accum_out=st[("s1", u)][:, n : n + 1]
+        def a_matmul(u, n):
+            acc = ps.tile([P, BANK], F32, tag="x", bufs=5)
+            for j in range(4):
+                t = 4 * n + j
+                nc.tensor.matmul(
+                    out=acc[:, j * P : (j + 1) * P], lhsT=bcol[:, t : t + 1].to_broadcast([P, P]), rhs=ident_f[:],
+                    is_transpose=True, start=(j == 0), stop=False,
                 )
+            nc.tensor.matmul(
+                out=acc[:], lhsT=xsT[:, u * P : (u + 1) * P], rhs=wT[:, n * BANK : (n + 1) * BANK],
+                start=False, stop=True,
+            )
+            a_banks[(u, n)] = acc
+
+        r_banks = {}
+
+        def r_matmul(u, n):
+            rows = slice(u * P, (u + 1) * P)
+            cols = slice(n * BANK, (n + 1) * BANK)
+            acc = ps.tile([P, BANK], F32, tag="r", bufs=3)
+            for c in range(2):
+                nc.tensor.matmul_mx(
+                    out=acc[:],
+                    lhsT=h_codes[:, c, rows].bitcast(FP8X4),
+                    lhsT_scale=h_scales[:, c, rows],
+                    rhs=w_codes[:, c, cols].bitcast(FP8X4),
+                    rhs_scale=w_scales[:, c, cols],
+                    start=(c == 0),
+                    stop=(c == 1),
+                )
+            r_banks[(u, n)] = acc
+
+        def r_evict(u, n, on_vector=False):
+            cols = slice(n * BANK, (n + 1) * BANK)
+            acc = r_banks[(u, n)]
+            s1 = st[("s1", u)][:, n : n + 1]
+            if on_vector:
+                nc.vector.tensor_scalar(
+                    out=r_tiles[u][:, cols], in0=acc[:], scalar1=1.0, scalar2=None, op0=ALU.mult, op1=ALU.add,
+                    accum_out=s1,
+                )
+            else:
+                nc.scalar.activation(out=r_tiles[u][:, cols], in_=acc[:], func=ACT.Identity, accum_out=s1)
 
         def r_mean(u):
             s1junk = small.tile([P, NB], F32, tag="s1junk")
@@ -248,22 +254,23 @@ def tile_multilstm_pa_kernel(
             nc.scalar.activation(
                 out=s1junk[:], in_=st[("s1", u)][:], func=ACT.Identity, scale=-1.0 / G, accum_out=negmean[:]
             )
-            ssq = small.tile([P, 2], F32, tag="ssq")
+            ssq = small.tile([P, 4], F32, tag="ssq")
             st[("negmean", u)] = negmean
             st[("ssq", u)] = ssq
 
         def r_var(u, k):
             junk = grp_pool.tile([P, 2048], BF16, tag="grp", align_bytes=64)
             nc.scalar.activation(
-                out=junk[:], in_=r_tiles[u][:, k * 2048 : (k + 1) * 2048], func=ACT.Square,
+                out=junk[:, 0:H], in_=r_tiles[u][:, k * H : (k + 1) * H], func=ACT.Square,
                 bias=st[("negmean", u)][:, 0:1], scale=1.0, accum_out=st[("ssq", u)][:, k : k + 1],
             )
-            if k == 1:
+            st[("nvar", u)] = st.get(("nvar", u), 0) + 1
+            if st[("nvar", u)] == 4:
                 ssq = st[("ssq", u)]
-                vjunk = small.tile([P, 2], F32, tag="vjunk")
+                vjunk = small.tile([P, 4], F32, tag="vjunk")
                 veps = small.tile([P, 1], F32, tag="veps")
                 nc.scalar.activation(
-                    out=vjunk[:], in_=ssq[:], func=ACT.Identity, bias=EPS / 2.0, scale=1.0 / G, accum_out=veps[:]
+                    out=vjunk[:], in_=ssq[:], func=ACT.Identity, bias=EPS / 4.0, scale=1.0 / G, accum_out=veps[:]
                 )
                 rstd = small.tile([P, 1], F32, tag="rstd")
                 nc.gpsimd.tensor_tensor(out=rstd[:], in0=veps[:], in1=neghalf[:, 0:1], op=ALU.pow)
@@ -279,24 +286,24 @@ def tile_multilstm_pa_kernel(
         funcs = [ACT.Sigmoid, ACT.Sigmoid, ACT.Tanh, ACT.Sigmoid]
 
         def c2(u, k):
-            cols = slice(k * H, (k + 1) * H)
-            nc.vector.scalar_tensor_tensor(
-                out=r_tiles[u][:, cols], in0=r_tiles[u][:, cols], scalar=st[("rstd", u)][:, 0:1],
-                in1=a_tiles[u][:, cols], op0=ALU.mult, op1=ALU.add,
-            )
-            nc.scalar.activation(out=r_tiles[u][:, cols], in_=r_tiles[u][:, cols], func=funcs[k])
+            for n in (2 * k, 2 * k + 1):
+                cols = slice(n * BANK, (n + 1) * BANK)
+                nc.vector.scalar_tensor_tensor(
+                    out=r_tiles[u][:, cols], in0=r_tiles[u][:, cols], scalar=st[("rstd", u)][:, 0:1],
+                    in1=a_banks[(u, n)][:], op0=ALU.mult, op1=ALU.add,
+                )
+            nc.scalar.activation(out=gate(u, k), in_=gate(u, k), func=funcs[k])
 
         def gate(u, k):
             return r_tiles[u][:, k * H : (k + 1) * H]
 
-        def side(u):
-            return nc.gpsimd if u in POOL_UNITS else nc.vector
-
         def m1(u):
-            side(u).tensor_tensor(out=gate(u, 1), in0=gate(u, 1), in1=c0_sb[:, u, :], op=ALU.mult)
+            nc.gpsimd.tensor_tensor(out=gate(u, 1), in0=gate(u, 1), in1=c0_sb[:, u, :], op=ALU.mult)
 
-        def m2_cp(u):
+        def m2(u):
             nc.vector.tensor_tensor(out=gate(u, 0), in0=gate(u, 0), in1=gate(u, 2), op=ALU.mult)
+
+        def cp(u):
             csum = small.tile([P, 1], F32, tag="csum")
             nc.vector.scalar_tensor_tensor(
                 out=gate(u, 0), in0=gate(u, 0), scalar=1.0, in1=gate(u, 1), op0=ALU.mult, op1=ALU.add,
@@ -353,86 +360,115 @@ def tile_multilstm_pa_kernel(
             nc.scalar.activation(out=gate(u, 0), in_=gate(u, 1), func=ACT.Tanh)
 
         def hy(u):
-            side(u).tensor_tensor(out=gate(u, 3), in0=gate(u, 3), in1=gate(u, 0), op=ALU.mult)
+            nc.gpsimd.tensor_tensor(out=gate(u, 3), in0=gate(u, 3), in1=gate(u, 0), op=ALU.mult)
             nc.sync.dma_start(out=out_0[u * P : (u + 1) * P, :], in_=gate(u, 3))
 
-        for k in range(A_BANKS):
-            a_matmul(k)
-        t1_group(0)
-        transpose_rows("h", h0_sb[:].bitcast(F32))
-        c0_sb = ld.tile([P, UNITS, H], BF16, tag="ld")
-        nc.sync.dma_start(out=c0_sb[:], in_=c0.rearrange("(u p) k -> p u k", p=P))
-        prep_whh(0)
-        t1_group(1)
-        quantise("h", h_codes, h_scales)
-        prep_whh(1)
-        c1(0)
-        quantise_whh(0)
-        prep_whh(2)
-        c1(1)
-        for g in range(2, 5):
-            quantise_whh(2 * g - 3)
-            prep_whh(2 * g - 1)
-            t1_group(g)
-            quantise_whh(2 * g - 2)
-            if 2 * g < NB:
-                prep_whh(2 * g)
-            c1(g)
-        quantise_whh(7)
-        r_evict(0, range(NB))
+        for q in range(4):
+            prep_wT(q)
+        transpose_rows("h", h0_sb[:].bitcast(F32), (1, 3))
+        prep_xs()
+        for n in range(NB + 2):
+            if n == 0:
+                quantise("h", h_codes, h_scales)
+            elif n <= NB:
+                quantise_whh(n - 1)
+            if n >= 2:
+                r_matmul(0, n - 2)
+                r_matmul(1, n - 2)
+                r_evict(0, n - 2)
+                r_evict(1, n - 2, on_vector=True)
+            if n < NB:
+                if n == 2:
+                    load_rest()
+                    prep_bias()
+                transpose_rows(n, whh_words[n], (3,))
         r_mean(0)
-        t1_group(5)
-        c1(5)
-        t1_group(6)
-        r_var(0, 0)
-        r_var(0, 1)
-        r_evict(1, range(NB))
         r_mean(1)
-        c1(6)
-        t1_group(7)
-        r_var(1, 0)
-        r_var(1, 1)
-        c1(7)
+        ORDER = (2, 3, 0, 1, 4, 5, 6, 7)
+        A_SEQ = [(u, n) for u in range(UNITS) for n in ORDER]
+        a_next = [0]
 
-        for k in range(4):
+        def a_more(count):
+            for u, n in A_SEQ[a_next[0] : a_next[0] + count]:
+                a_matmul(u, n)
+            a_next[0] += count
+
+        M_SEQ = [(u, n) for u in (2, 3) for n in range(NB)]
+        m_next = [0]
+
+        def m_more(count):
+            for u, n in M_SEQ[m_next[0] : m_next[0] + count]:
+                r_matmul(u, n)
+            m_next[0] += count
+
+        e_next = [0]
+
+        def e_more(count):
+            for u, n in M_SEQ[e_next[0] : e_next[0] + count]:
+                if n == 0:
+                    r_open(u)
+                r_evict(u, n)
+                m_more(1)
+                if n == NB - 1:
+                    r_mean(u)
+            e_next[0] += count
+
+        a_more(2)
+        m_more(3)
+        a_more(3)
+        for k in (1, 0, 2, 3):
+            r_var(0, k)
             t2(0, k)
-        for u in range(UNITS - 1):
-            far = u + 2 < UNITS
+        r_var(1, 1)
+        r_var(1, 0)
+
+        V_SEQ = [(u, k) for u in (1, 2, 3) for k in (1, 0, 2, 3)][2:]
+        v_next = [0]
+
+        def v_more(count):
+            for u, k in V_SEQ[v_next[0] : v_next[0] + count]:
+                r_var(u, k)
+            v_next[0] += count
+
+        AHEAD = [[(0, 2), (2, 0), (2, 0), (2, 0), (2, 0)], [(0, 2), (0, 2), (2, 0), (2, 0), (2, 0)], [(2, 1), (0, 1), (0, 1), (0, 1), (0, 0)], [(0, 0)] * 5]
+
+        def ahead(u, i):
+            ne, nv = AHEAD[u][i]
+            e_more(ne)
+            v_more(nv)
+
+        for u in range(UNITS):
+            last = u == UNITS - 1
             c2(u, 1)
+            a_more(2)
             c2(u, 0)
-            c2(u, 2)
-            c2(u, 3)
+            a_more(2)
+            ahead(u, 0)
             if u > 0:
                 hy(u - 1)
-            if far:
-                r_evict(u + 2, range(0, 6))
-            t2(u + 1, 0)
-            t2(u + 1, 1)
+            c2(u, 2)
             m1(u)
-            m2_cp(u)
+            a_more(2)
+            if not last:
+                t2(u + 1, 1)
+            c2(u, 3)
+            a_more(2)
+            ahead(u, 1)
+            m2(u)
+            cp(u)
+            if not last:
+                t2(u + 1, 0)
             c_var(u)
-            if far:
-                r_evict(u + 2, range(6, NB))
-                r_mean(u + 2)
-            t2(u + 1, 2)
+            ahead(u, 2)
             cy1(u)
-            t2(u + 1, 3)
-            if far:
-                r_var(u + 2, 0)
-            cy(u)
-            c_tanh(u)
-            if far:
-                r_var(u + 2, 1)
+            if not last:
+                t2(u + 1, 2)
+                cy(u)
+                ahead(u, 3)
+                c_tanh(u)
+                ahead(u, 4)
+                t2(u + 1, 3)
         last = UNITS - 1
-        c2(last, 1)
-        c2(last, 0)
-        c2(last, 2)
-        c2(last, 3)
-        m1(last)
-        m2_cp(last)
-        c_var(last)
-        cy1(last)
-        hy(last - 1)
         cy_half(last, 0)
         cy_half(last, 1)
         hy_half(last, 0)

@@ -41,38 +41,33 @@ def tile_multilstm_pa_kernel(
         nc.vector.memset(brow[64:128, :], 0.0)
         neghalf = const.tile([P, UNITS], F32)
         nc.vector.memset(neghalf[:], -0.5)
-
         x_sb = const.tile([P, UNITS, V], BF16)
-        nc.sync.dma_start(out=x_sb[:], in_=x.rearrange("(u p) v -> p u v", p=P))
-        for q in range(4):
+        wi_b = const.tile([P, G], BF16)
+        wh_b = const.tile([P, G], BF16)
+        h0_sb = const.tile([P, UNITS, H], BF16)
+        c0_sb = const.tile([P, UNITS, H], BF16)
+        lwlb = const.tile([P, 2, H], BF16)
+        whh_words = {}
+        r_tiles = {}
+        st = {}
+
+        def load_whh(n):
+            if n % 2 == 0:
+                wland = big.tile([P, 8, H], BF16, tag="big")
+                whh_words[n] = wland[:, 0:4, :]
+                whh_words[n + 1] = wland[:, 4:8, :]
+            nc.sync.dma_start(
+                out=whh_words[n], in_=w_hh1[n * BANK : (n + 1) * BANK, :].rearrange("(t p) k -> p t k", p=P)
+            )
+
+        def load_x():
+            nc.sync.dma_start(out=x_sb[:], in_=x.rearrange("(u p) v -> p u v", p=P))
+
+        def load_wih(q):
             nc.sync.dma_start(
                 out=wih_sb[:, 8 * q : 8 * q + 8, 0:V],
                 in_=w_ih1[q * 1024 : (q + 1) * 1024, :].rearrange("(t p) v -> p t v", p=P),
             )
-        wi_b = const.tile([P, G], BF16)
-        nc.sync.dma_start(out=wi_b[:], in_=lni_w1.partition_broadcast(P))
-        h0_sb = const.tile([P, UNITS, H], BF16)
-        nc.sync.dma_start(out=h0_sb[:], in_=h0.rearrange("(u p) k -> p u k", p=P))
-        whh_words = {}
-
-        def load_whh(m):
-            wland = big.tile([P, 8, H], BF16, tag="big")
-            for hh in range(2):
-                n = 2 * m + hh
-                nc.sync.dma_start(
-                    out=wland[:, 4 * hh : 4 * hh + 4, :],
-                    in_=w_hh1[n * BANK : (n + 1) * BANK, :].rearrange("(t p) k -> p t k", p=P),
-                )
-                whh_words[n] = wland[:].bitcast(F32)[:, 4 * hh : 4 * hh + 4, :]
-
-        load_whh(0)
-        nc.sync.dma_start(out=brow[0:32, :], in_=lni_b1.rearrange("(t p) -> t p", p=P))
-        nc.sync.dma_start(out=brow[32:64, :], in_=lnh_b1.rearrange("(t p) -> t p", p=P))
-        load_whh(1)
-        load_whh(2)
-        wh_b = const.tile([P, G], BF16)
-        r_tiles = {}
-        st = {}
 
         def r_open(u):
             r_new = big.tile([P, G], F32, tag="big")
@@ -80,13 +75,23 @@ def tile_multilstm_pa_kernel(
             s1 = small.tile([P, NB], F32, tag="s1")
             st[("s1", u)] = s1
 
+        nc.sync.dma_start(out=brow[0:32, :], in_=lni_b1.rearrange("(t p) -> t p", p=P))
+        nc.sync.dma_start(out=brow[32:64, :], in_=lnh_b1.rearrange("(t p) -> t p", p=P))
+        load_x()
+        for q in range(4):
+            load_wih(q)
+        nc.sync.dma_start(out=h0_sb[:], in_=h0.rearrange("(u p) k -> p u k", p=P))
+        for n in range(2):
+            load_whh(n)
+        nc.sync.dma_start(out=wi_b[:], in_=lni_w1.partition_broadcast(P))
+        for n in range(2, 6):
+            load_whh(n)
         r_open(0)
         r_open(1)
-        c0_sb = const.tile([P, UNITS, H], BF16)
-        lwlb = const.tile([P, 2, H], BF16)
 
         def load_rest():
-            load_whh(3)
+            load_whh(6)
+            load_whh(7)
             nc.sync.dma_start(out=wh_b[:], in_=lnh_w1.partition_broadcast(P))
             nc.sync.dma_start(out=c0_sb[:], in_=c0.rearrange("(u p) k -> p u k", p=P))
             nc.sync.dma_start(out=lwlb[:, 0, :], in_=lnc_w1.partition_broadcast(P))
@@ -97,42 +102,64 @@ def tile_multilstm_pa_kernel(
         ident_f = const.tile([P, P], F32)
         make_identity(nc, ident_f[:])
 
-        xT_f = const.tile([P, B], F32)
-        tpx = ps.tile([P, UNITS, P], BF16, tag="r", bufs=3)
-        for u in range(UNITS):
-            nc.tensor.transpose(tpx[:, u, :], x_sb[:, u, :], ident_b[:])
-        nc.scalar.copy(out=xT_f[:], in_=tpx[:].rearrange("p u b -> p (u b)"))
-        gram_ps = ps.tile([P, V + 1], F32, tag="r", bufs=3)
-        for t in range(GT):
-            nc.tensor.matmul(
-                out=gram_ps[:], lhsT=wih_sb[:, t, 0:V], rhs=wih_sb[:, t, 0 : V + 1], start=(t == 0), stop=(t == GT - 1)
-            )
-        gram = const.tile([P, V + 1], F32)
-        nc.scalar.copy(out=gram[:], in_=gram_ps[:])
-        wneg = const.tile([P, 1], F32)
-        nc.scalar.activation(out=wneg[:], in_=gram[:, V : V + 1], func=ACT.Identity, scale=-1.0 / G)
+        tpb = ps.tile([P, P], BF16, tag="r", bufs=3)
+        nc.tensor.transpose(tpb[:], brow[:], ident_b[:])
+        b2 = const.tile([P, 2 * GT], F32)
+        nc.scalar.copy(out=b2[:], in_=tpb[:, 0 : 2 * GT])
+        bcol = const.tile([P, GT], F32)
+        nc.vector.tensor_tensor(out=bcol[:], in0=b2[:, 0:GT], in1=b2[:, GT : 2 * GT], op=ALU.add)
+        bwide = const.tile([P, GT, P], F32)
+        nc.vector.tensor_copy(out=bwide[:], in_=bcol[:].unsqueeze(2).to_broadcast([P, GT, P]))
 
-        q4 = const.tile([P, UNITS], F32)
-        mean4 = const.tile([P, UNITS], F32)
-        for u in range(UNITS):
-            y_ps = ps.tile([P, V + 1], F32, tag="r", bufs=3)
-            nc.tensor.matmul(out=y_ps[:], lhsT=xT_f[:, u * P : (u + 1) * P], rhs=gram[:], start=True, stop=True)
-            yjunk = small.tile([P, V], F32, tag="yjunk")
-            nc.vector.scalar_tensor_tensor(
-                out=yjunk[:], in0=y_ps[:, 0:V], scalar=1.0 / G, in1=x_sb[:, u, :], op0=ALU.mult, op1=ALU.mult,
-                accum_out=q4[:, u : u + 1],
-            )
-            nc.vector.tensor_scalar(
-                out=mean4[:, u : u + 1], in0=y_ps[:, V : V + 1], scalar1=1.0 / G, scalar2=None, op0=ALU.mult
-            )
-        msq4 = const.tile([P, UNITS], F32)
-        nc.vector.tensor_tensor(out=msq4[:], in0=mean4[:], in1=mean4[:], op=ALU.mult)
-        var4 = const.tile([P, UNITS], F32)
-        nc.vector.tensor_tensor(out=var4[:], in0=q4[:], in1=msq4[:], op=ALU.subtract)
-        veps4 = const.tile([P, UNITS], F32)
-        nc.gpsimd.tensor_scalar(out=veps4[:], in0=var4[:], scalar1=0.0, scalar2=EPS, op0=ALU.max, op1=ALU.add)
+        xT_f = const.tile([P, B], F32)
+        gram = const.tile([P, V + 1], F32)
+        wneg = const.tile([P, 1], F32)
         rstd4 = const.tile([P, UNITS], F32)
-        nc.gpsimd.tensor_tensor(out=rstd4[:], in0=veps4[:], in1=neghalf[:], op=ALU.pow)
+
+        def x_transposes():
+            tpx = ps.tile([P, UNITS, P], BF16, tag="r", bufs=3)
+            for u in range(UNITS):
+                nc.tensor.transpose(tpx[:, u, :], x_sb[:, u, :], ident_b[:])
+            nc.scalar.copy(out=xT_f[:], in_=tpx[:].rearrange("p u b -> p (u b)"))
+
+        def gram_matrix():
+            gram_ps = ps.tile([P, V + 1], F32, tag="r", bufs=3)
+            for t in range(GT):
+                nc.tensor.matmul(
+                    out=gram_ps[:], lhsT=wih_sb[:, t, 0:V], rhs=wih_sb[:, t, 0 : V + 1],
+                    start=(t == 0), stop=(t == GT - 1),
+                )
+            nc.scalar.copy(out=gram[:], in_=gram_ps[:])
+            nc.scalar.activation(out=wneg[:], in_=gram[:, V : V + 1], func=ACT.Identity, scale=-1.0 / G)
+
+        def a_stats():
+            q4 = const.tile([P, UNITS], F32)
+            mean4 = const.tile([P, UNITS], F32)
+            y_ps = {}
+            for g in range(2):
+                y_new = ps.tile([P, 2, 256], F32, tag="r", bufs=3)
+                for i in range(2):
+                    u = 2 * g + i
+                    nc.tensor.matmul(
+                        out=y_new[:, i, 0 : V + 1], lhsT=xT_f[:, u * P : (u + 1) * P], rhs=gram[:], start=True, stop=True
+                    )
+                    y_ps[u] = y_new[:, i, :]
+            for u in range(UNITS):
+                yjunk = small.tile([P, V], F32, tag="yjunk")
+                nc.vector.scalar_tensor_tensor(
+                    out=yjunk[:], in0=y_ps[u][:, 0:V], scalar=1.0 / G, in1=x_sb[:, u, :], op0=ALU.mult, op1=ALU.mult,
+                    accum_out=q4[:, u : u + 1],
+                )
+                nc.vector.tensor_scalar(
+                    out=mean4[:, u : u + 1], in0=y_ps[u][:, V : V + 1], scalar1=1.0 / G, scalar2=None, op0=ALU.mult
+                )
+            msq4 = const.tile([P, UNITS], F32)
+            nc.vector.tensor_tensor(out=msq4[:], in0=mean4[:], in1=mean4[:], op=ALU.mult)
+            var4 = const.tile([P, UNITS], F32)
+            nc.vector.tensor_tensor(out=var4[:], in0=q4[:], in1=msq4[:], op=ALU.subtract)
+            veps4 = const.tile([P, UNITS], F32)
+            nc.gpsimd.tensor_scalar(out=veps4[:], in0=var4[:], scalar1=0.0, scalar2=EPS, op0=ALU.max, op1=ALU.add)
+            nc.gpsimd.tensor_tensor(out=rstd4[:], in0=veps4[:], in1=neghalf[:], op=ALU.pow)
 
         h_codes = const.tile([P, 2, B], U32, align_bytes=64)
         h_scales = const.tile([P, 2, B], U8, align_bytes=64)
@@ -141,7 +168,6 @@ def tile_multilstm_pa_kernel(
         wT = const.tile([P, G], F32)
         xs = const.tile([P, UNITS, V], F32)
         xsT = const.tile([P, B], F32)
-        bcol = const.tile([P, GT], F32)
         grp_tiles = {}
 
         def transpose_rows(key, src_words, on_vector):
@@ -185,13 +211,6 @@ def tile_multilstm_pa_kernel(
                 op0=ALU.add, op1=ALU.mult,
             )
 
-        def prep_bias():
-            tpb = ps.tile([P, P], BF16, tag="r", bufs=3)
-            nc.tensor.transpose(tpb[:], brow[:], ident_b[:])
-            b2 = const.tile([P, 64], F32)
-            nc.scalar.copy(out=b2[:], in_=tpb[:, 0:64])
-            nc.vector.tensor_tensor(out=bcol[:], in0=b2[:, 0:GT], in1=b2[:, GT : 2 * GT], op=ALU.add)
-
         def prep_xs():
             for u in range(UNITS):
                 nc.vector.tensor_scalar(
@@ -209,7 +228,7 @@ def tile_multilstm_pa_kernel(
             for j in range(4):
                 t = 4 * n + j
                 nc.tensor.matmul(
-                    out=acc[:, j * P : (j + 1) * P], lhsT=bcol[:, t : t + 1].to_broadcast([P, P]), rhs=ident_f[:],
+                    out=acc[:, j * P : (j + 1) * P], lhsT=bwide[:, t, :], rhs=ident_f[:],
                     is_transpose=True, start=(j == 0), stop=False,
                 )
             nc.tensor.matmul(
@@ -236,17 +255,33 @@ def tile_multilstm_pa_kernel(
                 )
             r_banks[(u, n)] = acc
 
-        def r_evict(u, n, on_vector=False):
+        def r_evict(u, n):
             cols = slice(n * BANK, (n + 1) * BANK)
-            acc = r_banks[(u, n)]
             s1 = st[("s1", u)][:, n : n + 1]
+            nc.scalar.activation(out=r_tiles[u][:, cols], in_=r_banks[(u, n)][:], func=ACT.Identity, accum_out=s1)
+
+        def r_copy(u, n, on_vector=False):
+            cols = slice(n * BANK, (n + 1) * BANK)
             if on_vector:
-                nc.vector.tensor_scalar(
-                    out=r_tiles[u][:, cols], in0=acc[:], scalar1=1.0, scalar2=None, op0=ALU.mult, op1=ALU.add,
-                    accum_out=s1,
-                )
+                nc.vector.tensor_copy(out=r_tiles[u][:, cols], in_=r_banks[(u, n)][:])
             else:
-                nc.scalar.activation(out=r_tiles[u][:, cols], in_=acc[:], func=ACT.Identity, accum_out=s1)
+                nc.scalar.copy(out=r_tiles[u][:, cols], in_=r_banks[(u, n)][:])
+
+        def r_stats(u, n):
+            if n == 0:
+                bst = small.tile([P, NB, 6], F32, tag="bst")
+                st[("bst", u)] = bst
+            nc.vector.bn_stats(out=st[("bst", u)][:, n, :], in_=r_tiles[u][:, n * BANK : (n + 1) * BANK])
+
+        def r_stats_end(u):
+            mv = small.tile([P, 2], F32, tag="mv")
+            nc.vector.bn_aggr(out=mv[:], in_=st[("bst", u)][:].rearrange("p n s -> p (n s)"))
+            veps = small.tile([P, 1], F32, tag="veps")
+            nc.gpsimd.tensor_scalar(out=veps[:], in0=mv[:, 1:2], scalar1=0.0, scalar2=EPS, op0=ALU.max, op1=ALU.add)
+            rstd = small.tile([P, 1], F32, tag="rstd")
+            nc.gpsimd.tensor_tensor(out=rstd[:], in0=veps[:], in1=neghalf[:, 0:1], op=ALU.pow)
+            st[("mean", u)] = mv
+            st[("rstd", u)] = rstd
 
         def r_mean(u):
             s1junk = small.tile([P, NB], F32, tag="s1junk")
@@ -278,9 +313,13 @@ def tile_multilstm_pa_kernel(
 
         def t2(u, k):
             cols = slice(k * H, (k + 1) * H)
+            if ("mean", u) in st:
+                centre, op = st[("mean", u)], ALU.subtract
+            else:
+                centre, op = st[("negmean", u)], ALU.add
             nc.vector.scalar_tensor_tensor(
-                out=r_tiles[u][:, cols], in0=r_tiles[u][:, cols], scalar=st[("negmean", u)][:, 0:1],
-                in1=wh_b[:, cols], op0=ALU.add, op1=ALU.mult,
+                out=r_tiles[u][:, cols], in0=r_tiles[u][:, cols], scalar=centre[:, 0:1],
+                in1=wh_b[:, cols], op0=op, op1=ALU.mult,
             )
 
         funcs = [ACT.Sigmoid, ACT.Sigmoid, ACT.Tanh, ACT.Sigmoid]
@@ -363,28 +402,37 @@ def tile_multilstm_pa_kernel(
             nc.gpsimd.tensor_tensor(out=gate(u, 3), in0=gate(u, 3), in1=gate(u, 0), op=ALU.mult)
             nc.sync.dma_start(out=out_0[u * P : (u + 1) * P, :], in_=gate(u, 3))
 
-        for q in range(4):
-            prep_wT(q)
-        transpose_rows("h", h0_sb[:].bitcast(F32), (1, 3))
-        prep_xs()
-        for n in range(NB + 2):
+        def words(ap):
+            return ap.bitcast(F32)
+
+        WT_AT = {2: (0,), 3: (1,), 4: (2,), 5: (3,)}
+        V_COPIES = {}
+        x_transposes()
+        gram_matrix()
+        a_stats()
+        transpose_rows("h", words(h0_sb[:]), (1, 3))
+        for n in range(NB + 3):
             if n == 0:
                 quantise("h", h_codes, h_scales)
             elif n <= NB:
                 quantise_whh(n - 1)
-            if n >= 2:
-                r_matmul(0, n - 2)
-                r_matmul(1, n - 2)
-                r_evict(0, n - 2)
-                r_evict(1, n - 2, on_vector=True)
+            if 2 <= n < NB + 2:
+                for u in range(2):
+                    r_matmul(u, n - 2)
+                for u in range(2):
+                    r_copy(u, n - 2)
+            if n == 2:
+                load_rest()
             if n < NB:
-                if n == 2:
-                    load_rest()
-                    prep_bias()
-                transpose_rows(n, whh_words[n], (3,))
-        r_mean(0)
-        r_mean(1)
-        ORDER = (2, 3, 0, 1, 4, 5, 6, 7)
+                transpose_rows(n, words(whh_words[n]), V_COPIES.get(n, ()))
+            for q in WT_AT.get(n, ()):
+                prep_wT(q)
+            if n == 1:
+                prep_xs()
+            if n >= 3:
+                for u in range(2):
+                    r_stats(u, n - 3)
+        ORDER = (2, 3, 4, 5, 0, 1, 6, 7)
         A_SEQ = [(u, n) for u in range(UNITS) for n in ORDER]
         a_next = [0]
 
@@ -413,16 +461,7 @@ def tile_multilstm_pa_kernel(
                     r_mean(u)
             e_next[0] += count
 
-        a_more(2)
-        m_more(3)
-        a_more(3)
-        for k in (1, 0, 2, 3):
-            r_var(0, k)
-            t2(0, k)
-        r_var(1, 1)
-        r_var(1, 0)
-
-        V_SEQ = [(u, k) for u in (1, 2, 3) for k in (1, 0, 2, 3)][2:]
+        V_SEQ = [(u, k) for u in (2, 3) for k in (1, 2, 0, 3)]
         v_next = [0]
 
         def v_more(count):
@@ -430,45 +469,60 @@ def tile_multilstm_pa_kernel(
                 r_var(u, k)
             v_next[0] += count
 
-        AHEAD = [[(0, 2), (2, 0), (2, 0), (2, 0), (2, 0)], [(0, 2), (0, 2), (2, 0), (2, 0), (2, 0)], [(2, 1), (0, 1), (0, 1), (0, 1), (0, 0)], [(0, 0)] * 5]
-
         def ahead(u, i):
             ne, nv = AHEAD[u][i]
             e_more(ne)
             v_more(nv)
 
+        AHEAD = [[(2, 0), (1, 0), (1, 0), (1, 0), (2, 0)], [(1, 2), (1, 1), (1, 1), (1, 0), (2, 0)], [(3, 1), (0, 1), (0, 1), (0, 1), (0, 0)], [(0, 0)] * 5]
+        a_more(3)
+        m_more(2)
+        a_more(5 - 3)
+        r_stats_end(0)
+        r_stats_end(1)
+        t2(0, 1)
+        t2(0, 2)
+
         for u in range(UNITS):
             last = u == UNITS - 1
+            first = u == 0
             c2(u, 1)
             a_more(2)
-            c2(u, 0)
-            a_more(2)
-            ahead(u, 0)
-            if u > 0:
-                hy(u - 1)
-            c2(u, 2)
             m1(u)
+            if first:
+                t2(0, 0)
+            ahead(u, 0)
+            if not first:
+                cy1(u - 1)
+            c2(u, 2)
             a_more(2)
+            if first:
+                t2(0, 3)
+            else:
+                cy(u - 1)
+                c_tanh(u - 1)
             if not last:
                 t2(u + 1, 1)
-            c2(u, 3)
-            a_more(2)
             ahead(u, 1)
-            m2(u)
-            cp(u)
-            if not last:
-                t2(u + 1, 0)
-            c_var(u)
+            c2(u, 0)
+            a_more(2)
+            if not first:
+                hy(u - 1)
             ahead(u, 2)
-            cy1(u)
             if not last:
                 t2(u + 1, 2)
-                cy(u)
-                ahead(u, 3)
-                c_tanh(u)
+            m2(u)
+            c2(u, 3)
+            a_more(2)
+            ahead(u, 3)
+            cp(u)
+            c_var(u)
+            if not last:
+                t2(u + 1, 0)
                 ahead(u, 4)
                 t2(u + 1, 3)
         last = UNITS - 1
+        cy1(last)
         cy_half(last, 0)
         cy_half(last, 1)
         hy_half(last, 0)

@@ -337,7 +337,7 @@ def tile_multilstm_pa_kernel(
             return r_tiles[u][:, k * H : (k + 1) * H]
 
         def m1(u):
-            nc.gpsimd.tensor_tensor(out=gate(u, 1), in0=gate(u, 1), in1=c0_sb[:, u, :], op=ALU.mult)
+            nc.vector.tensor_tensor(out=gate(u, 1), in0=gate(u, 1), in1=c0_sb[:, u, :], op=ALU.mult)
 
         def m2(u):
             nc.vector.tensor_tensor(out=gate(u, 0), in0=gate(u, 0), in1=gate(u, 2), op=ALU.mult)
@@ -399,7 +399,7 @@ def tile_multilstm_pa_kernel(
             nc.scalar.activation(out=gate(u, 0), in_=gate(u, 1), func=ACT.Tanh)
 
         def hy(u):
-            nc.gpsimd.tensor_tensor(out=gate(u, 3), in0=gate(u, 3), in1=gate(u, 0), op=ALU.mult)
+            nc.vector.tensor_tensor(out=gate(u, 3), in0=gate(u, 3), in1=gate(u, 0), op=ALU.mult)
             nc.sync.dma_start(out=out_0[u * P : (u + 1) * P, :], in_=gate(u, 3))
 
         def words(ap):
@@ -474,7 +474,7 @@ def tile_multilstm_pa_kernel(
             e_more(ne)
             v_more(nv)
 
-        AHEAD = [[(2, 0), (1, 0), (1, 0), (1, 0), (2, 0)], [(1, 2), (1, 1), (1, 1), (1, 0), (2, 0)], [(3, 1), (0, 1), (0, 1), (0, 1), (0, 0)], [(0, 0)] * 5]
+        AHEAD = [[(1, 0), (1, 0), (2, 0), (2, 0), (2, 0)], [(0, 2), (1, 1), (1, 1), (2, 0), (2, 0)], [(2, 1), (0, 1), (0, 1), (0, 1), (0, 0)], [(0, 0)] * 5]
         a_more(3)
         m_more(2)
         a_more(5 - 3)
@@ -488,7 +488,6 @@ def tile_multilstm_pa_kernel(
             first = u == 0
             c2(u, 1)
             a_more(2)
-            m1(u)
             if first:
                 t2(0, 0)
             ahead(u, 0)
@@ -504,6 +503,7 @@ def tile_multilstm_pa_kernel(
             if not last:
                 t2(u + 1, 1)
             ahead(u, 1)
+            m1(u)
             c2(u, 0)
             a_more(2)
             if not first:
@@ -511,9 +511,9 @@ def tile_multilstm_pa_kernel(
             ahead(u, 2)
             if not last:
                 t2(u + 1, 2)
-            m2(u)
             c2(u, 3)
             a_more(2)
+            m2(u)
             ahead(u, 3)
             cp(u)
             c_var(u)

@@ -31,7 +31,9 @@ def tile_multilstm_pa_kernel(
         ctx.enter_context(tc.manual_schedule())
         const = ctx.enter_context(tc.tile_pool(name="const", bufs=1))
         grp_pool = ctx.enter_context(tc.tile_pool(name="grp", bufs=6))
-        big = ctx.enter_context(tc.tile_pool(name="big", bufs=5))
+        hc = ctx.enter_context(tc.tile_pool(name="hc", bufs=1))
+        land = ctx.enter_context(tc.tile_pool(name="land", bufs=3))
+        big = ctx.enter_context(tc.tile_pool(name="big", bufs=4))
         small = ctx.enter_context(tc.tile_pool(name="small", bufs=4))
         ps = ctx.enter_context(tc.psum_pool(name="ps", bufs=4))
 
@@ -44,20 +46,17 @@ def tile_multilstm_pa_kernel(
         x_sb = const.tile([P, UNITS, V], BF16)
         wi_b = const.tile([P, G], BF16)
         wh_b = const.tile([P, G], BF16)
-        h0_sb = const.tile([P, UNITS, H], BF16)
-        c0_sb = const.tile([P, UNITS, H], BF16)
+        h0_sb = hc.tile([P, UNITS, H], BF16, tag="hc")
         lwlb = const.tile([P, 2, H], BF16)
         whh_words = {}
         r_tiles = {}
         st = {}
 
         def load_whh(n):
-            if n % 2 == 0:
-                wland = big.tile([P, 8, H], BF16, tag="big")
-                whh_words[n] = wland[:, 0:4, :]
-                whh_words[n + 1] = wland[:, 4:8, :]
+            wland = land.tile([P, 4, H], BF16, tag="land")
+            whh_words[n] = wland[:]
             nc.sync.dma_start(
-                out=whh_words[n], in_=w_hh1[n * BANK : (n + 1) * BANK, :].rearrange("(t p) k -> p t k", p=P)
+                out=wland[:], in_=w_hh1[n * BANK : (n + 1) * BANK, :].rearrange("(t p) k -> p t k", p=P)
             )
 
         def load_x():
@@ -75,41 +74,50 @@ def tile_multilstm_pa_kernel(
             s1 = small.tile([P, NB], F32, tag="s1")
             st[("s1", u)] = s1
 
-        nc.sync.dma_start(out=brow[0:32, :], in_=lni_b1.rearrange("(t p) -> t p", p=P))
-        nc.sync.dma_start(out=brow[32:64, :], in_=lnh_b1.rearrange("(t p) -> t p", p=P))
         load_x()
         for q in range(4):
             load_wih(q)
+        nc.sync.dma_start(out=wi_b[:], in_=lni_w1.partition_broadcast(P))
         nc.sync.dma_start(out=h0_sb[:], in_=h0.rearrange("(u p) k -> p u k", p=P))
         for n in range(2):
             load_whh(n)
-        nc.sync.dma_start(out=wi_b[:], in_=lni_w1.partition_broadcast(P))
-        for n in range(2, 6):
-            load_whh(n)
-        r_open(0)
-        r_open(1)
+        load_whh(2)
+        for u in range(UNITS):
+            r_open(u)
 
-        def load_rest():
-            load_whh(6)
-            load_whh(7)
-            nc.sync.dma_start(out=wh_b[:], in_=lnh_w1.partition_broadcast(P))
-            nc.sync.dma_start(out=c0_sb[:], in_=c0.rearrange("(u p) k -> p u k", p=P))
-            nc.sync.dma_start(out=lwlb[:, 0, :], in_=lnc_w1.partition_broadcast(P))
-            nc.sync.dma_start(out=lwlb[:, 1, :], in_=lnc_b1.partition_broadcast(P))
+        def load_more(n):
+            if n < NB:
+                load_whh(n)
+            if n == 5:
+                nc.sync.dma_start(out=brow[0:32, :], in_=lni_b1.rearrange("(t p) -> t p", p=P))
+                nc.sync.dma_start(out=brow[32:64, :], in_=lnh_b1.rearrange("(t p) -> t p", p=P))
+            if n == NB:
+                nc.sync.dma_start(out=wh_b[:], in_=lnh_w1.partition_broadcast(P))
+                c0_new = hc.tile([P, UNITS, H], BF16, tag="hc")
+                st["c0"] = c0_new
+                nc.sync.dma_start(out=c0_new[:], in_=c0.rearrange("(u p) k -> p u k", p=P))
+                nc.sync.dma_start(out=lwlb[:, 0, :], in_=lnc_w1.partition_broadcast(P))
+                nc.sync.dma_start(out=lwlb[:, 1, :], in_=lnc_b1.partition_broadcast(P))
 
         ident_b = const.tile([P, P], BF16)
         make_identity(nc, ident_b[:])
         ident_f = const.tile([P, P], F32)
         make_identity(nc, ident_f[:])
 
-        tpb = ps.tile([P, P], BF16, tag="r", bufs=3)
-        nc.tensor.transpose(tpb[:], brow[:], ident_b[:])
-        b2 = const.tile([P, 2 * GT], F32)
-        nc.scalar.copy(out=b2[:], in_=tpb[:, 0 : 2 * GT])
-        bcol = const.tile([P, GT], F32)
-        nc.vector.tensor_tensor(out=bcol[:], in0=b2[:, 0:GT], in1=b2[:, GT : 2 * GT], op=ALU.add)
         bwide = const.tile([P, GT, P], F32)
-        nc.vector.tensor_copy(out=bwide[:], in_=bcol[:].unsqueeze(2).to_broadcast([P, GT, P]))
+
+        def prep_bias():
+            tpb = ps.tile([P, P], BF16, tag="r", bufs=4)
+            nc.tensor.transpose(tpb[:], brow[:], ident_b[:])
+            b2 = const.tile([P, 2 * GT], F32)
+            nc.scalar.copy(out=b2[:], in_=tpb[:, 0 : 2 * GT])
+            st["b2"] = b2
+
+        def spread_bias():
+            b2 = st["b2"]
+            bcol = const.tile([P, GT], F32)
+            nc.vector.tensor_tensor(out=bcol[:], in0=b2[:, 0:GT], in1=b2[:, GT : 2 * GT], op=ALU.add)
+            nc.vector.tensor_copy(out=bwide[:], in_=bcol[:].unsqueeze(2).to_broadcast([P, GT, P]))
 
         xT_f = const.tile([P, B], F32)
         gram = const.tile([P, V + 1], F32)
@@ -117,13 +125,13 @@ def tile_multilstm_pa_kernel(
         rstd4 = const.tile([P, UNITS], F32)
 
         def x_transposes():
-            tpx = ps.tile([P, UNITS, P], BF16, tag="r", bufs=3)
+            tpx = ps.tile([P, UNITS, P], BF16, tag="r", bufs=4)
             for u in range(UNITS):
                 nc.tensor.transpose(tpx[:, u, :], x_sb[:, u, :], ident_b[:])
             nc.scalar.copy(out=xT_f[:], in_=tpx[:].rearrange("p u b -> p (u b)"))
 
         def gram_matrix():
-            gram_ps = ps.tile([P, V + 1], F32, tag="r", bufs=3)
+            gram_ps = ps.tile([P, V + 1], F32, tag="r", bufs=4)
             for t in range(GT):
                 nc.tensor.matmul(
                     out=gram_ps[:], lhsT=wih_sb[:, t, 0:V], rhs=wih_sb[:, t, 0 : V + 1],
@@ -137,7 +145,7 @@ def tile_multilstm_pa_kernel(
             mean4 = const.tile([P, UNITS], F32)
             y_ps = {}
             for g in range(2):
-                y_new = ps.tile([P, 2, 256], F32, tag="r", bufs=3)
+                y_new = ps.tile([P, 2, 256], F32, tag="r", bufs=4)
                 for i in range(2):
                     u = 2 * g + i
                     nc.tensor.matmul(
@@ -170,19 +178,31 @@ def tile_multilstm_pa_kernel(
         xsT = const.tile([P, B], F32)
         grp_tiles = {}
 
+        perm_tiles = {}
+
+        def even_odd(key, src_words, engine):
+            new = hc.tile([P, 4, 2, 2, P], F32, tag="perm")
+            dst = new[:].rearrange("p r c s w -> p (r c) s w")
+            src = src_words.rearrange("p r (c w s) -> p (r c) s w", c=2, s=2)
+            if engine == "v":
+                nc.vector.tensor_copy(out=dst, in_=src)
+            else:
+                nc.scalar.copy(out=dst, in_=src)
+            perm_tiles[key] = new
+
         def transpose_rows(key, src_words, on_vector):
             for c in range(2):
                 grp = grp_pool.tile([P, 4 * BANK], BF16, tag="grp", align_bytes=64)
                 grpw = grp[:].bitcast(F32).rearrange("p (r s) -> p r s", s=2)
                 for half in range(2):
-                    tp = ps.tile([P, 2, 256], F32, tag="x", bufs=5)
+                    tp = ps.tile([P, 2, 256], F32, tag="x", bufs=4)
                     for s in range(2):
                         for j in range(2):
-                            nc.tensor.transpose(
-                                tp[:, s, j * P : (j + 1) * P],
-                                src_words[:, 2 * half + j, 256 * c + s : 256 * (c + 1) : 2],
-                                ident_f[:],
-                            )
+                            if key in perm_tiles:
+                                piece = perm_tiles[key][:, 2 * half + j, c, s, :]
+                            else:
+                                piece = src_words[:, 2 * half + j, 256 * c + s : 256 * (c + 1) : 2]
+                            nc.tensor.transpose(tp[:, s, j * P : (j + 1) * P], piece, ident_f[:])
                     dst = grpw[:, half * 256 : (half + 1) * 256, :]
                     src = tp[:].rearrange("p s r -> p r s")
                     if 2 * c + half in on_vector:
@@ -202,7 +222,7 @@ def tile_multilstm_pa_kernel(
             quantise(n, w_codes[:, :, cols], w_scales[:, :, cols])
 
         def prep_wT(q):
-            tpw = ps.tile([P, 8, P], BF16, tag="r", bufs=3)
+            tpw = ps.tile([P, 8, P], BF16, tag="r", bufs=4)
             for j in range(8):
                 nc.tensor.transpose(tpw[:, j, :], wih_sb[:, 8 * q + j, 0:V], ident_b[:])
             cols = slice(q * 1024, (q + 1) * 1024)
@@ -216,7 +236,7 @@ def tile_multilstm_pa_kernel(
                 nc.vector.tensor_scalar(
                     out=xs[:, u, :], in0=x_sb[:, u, :], scalar1=rstd4[:, u : u + 1], scalar2=None, op0=ALU.mult
                 )
-            tps = ps.tile([P, UNITS, P], F32, tag="r", bufs=3)
+            tps = ps.tile([P, UNITS, P], F32, tag="r", bufs=4)
             for u in range(UNITS):
                 nc.tensor.transpose(tps[:, u, :], xs[:, u, :], ident_f[:])
             nc.scalar.copy(out=xsT[:], in_=tps[:].rearrange("p u b -> p (u b)"))
@@ -224,7 +244,7 @@ def tile_multilstm_pa_kernel(
         a_banks = {}
 
         def a_matmul(u, n):
-            acc = ps.tile([P, BANK], F32, tag="x", bufs=5)
+            acc = ps.tile([P, BANK], F32, tag="x", bufs=4)
             for j in range(4):
                 t = 4 * n + j
                 nc.tensor.matmul(
@@ -242,7 +262,7 @@ def tile_multilstm_pa_kernel(
         def r_matmul(u, n):
             rows = slice(u * P, (u + 1) * P)
             cols = slice(n * BANK, (n + 1) * BANK)
-            acc = ps.tile([P, BANK], F32, tag="r", bufs=3)
+            acc = ps.tile([P, BANK], F32, tag="r", bufs=4)
             for c in range(2):
                 nc.tensor.matmul_mx(
                     out=acc[:],
@@ -255,9 +275,15 @@ def tile_multilstm_pa_kernel(
                 )
             r_banks[(u, n)] = acc
 
-        def r_evict(u, n):
+        def r_evict(u, n, on_vector=False):
             cols = slice(n * BANK, (n + 1) * BANK)
             s1 = st[("s1", u)][:, n : n + 1]
+            if on_vector:
+                nc.vector.tensor_scalar(
+                    out=r_tiles[u][:, cols], in0=r_banks[(u, n)][:], scalar1=1.0, scalar2=None, op0=ALU.mult, op1=ALU.add,
+                    accum_out=s1,
+                )
+                return
             nc.scalar.activation(out=r_tiles[u][:, cols], in_=r_banks[(u, n)][:], func=ACT.Identity, accum_out=s1)
 
         def r_copy(u, n, on_vector=False):
@@ -337,7 +363,7 @@ def tile_multilstm_pa_kernel(
             return r_tiles[u][:, k * H : (k + 1) * H]
 
         def m1(u):
-            nc.vector.tensor_tensor(out=gate(u, 1), in0=gate(u, 1), in1=c0_sb[:, u, :], op=ALU.mult)
+            nc.vector.tensor_tensor(out=gate(u, 1), in0=gate(u, 1), in1=st["c0"][:, u, :], op=ALU.mult)
 
         def m2(u):
             nc.vector.tensor_tensor(out=gate(u, 0), in0=gate(u, 0), in1=gate(u, 2), op=ALU.mult)
@@ -349,7 +375,7 @@ def tile_multilstm_pa_kernel(
                 accum_out=csum[:],
             )
             cneg = small.tile([P, 1], F32, tag="cneg")
-            nc.vector.tensor_scalar(out=cneg[:], in0=csum[:], scalar1=-1.0 / H, scalar2=None, op0=ALU.mult)
+            nc.scalar.activation(out=cneg[:], in_=csum[:], func=ACT.Identity, scale=-1.0 / H)
             st[("cneg", u)] = cneg
 
         def c_var(u):
@@ -405,12 +431,13 @@ def tile_multilstm_pa_kernel(
         def words(ap):
             return ap.bitcast(F32)
 
-        WT_AT = {2: (0,), 3: (1,), 4: (2,), 5: (3,)}
-        V_COPIES = {}
+        WT_AT = {}
         x_transposes()
         gram_matrix()
         a_stats()
-        transpose_rows("h", words(h0_sb[:]), (1, 3))
+        for q in range(4):
+            prep_wT(q)
+        transpose_rows("h", words(h0_sb[:]), ())
         for n in range(NB + 3):
             if n == 0:
                 quantise("h", h_codes, h_scales)
@@ -420,15 +447,18 @@ def tile_multilstm_pa_kernel(
                 for u in range(2):
                     r_matmul(u, n - 2)
                 for u in range(2):
-                    r_copy(u, n - 2)
-            if n == 2:
-                load_rest()
+                    r_copy(u, n - 2, (n - 2, u) in ())
             if n < NB:
-                transpose_rows(n, words(whh_words[n]), V_COPIES.get(n, ()))
+                transpose_rows(n, words(whh_words[n]), ())
+                load_more(n + 3)
             for q in WT_AT.get(n, ()):
                 prep_wT(q)
-            if n == 1:
+            if n == 2:
                 prep_xs()
+            if n == 4:
+                prep_bias()
+            if n == 5:
+                spread_bias()
             if n >= 3:
                 for u in range(2):
                     r_stats(u, n - 3)
@@ -441,7 +471,11 @@ def tile_multilstm_pa_kernel(
                 a_matmul(u, n)
             a_next[0] += count
 
-        M_SEQ = [(u, n) for u in (2, 3) for n in range(NB)]
+        a_more(4)
+        for u in range(2):
+            r_stats_end(u)
+
+        M_SEQ = [(u, n) for u in range(2, UNITS) for n in range(NB)]
         m_next = [0]
 
         def m_more(count):
@@ -453,15 +487,13 @@ def tile_multilstm_pa_kernel(
 
         def e_more(count):
             for u, n in M_SEQ[e_next[0] : e_next[0] + count]:
-                if n == 0:
-                    r_open(u)
                 r_evict(u, n)
                 m_more(1)
                 if n == NB - 1:
                     r_mean(u)
             e_next[0] += count
 
-        V_SEQ = [(u, k) for u in (2, 3) for k in (1, 2, 0, 3)]
+        V_SEQ = [(u, k) for u in range(2, UNITS) for k in (1, 2, 0, 3)]
         v_next = [0]
 
         def v_more(count):
@@ -469,58 +501,44 @@ def tile_multilstm_pa_kernel(
                 r_var(u, k)
             v_next[0] += count
 
-        def ahead(u, i):
-            ne, nv = AHEAD[u][i]
+        def ahead(ne, nv):
             e_more(ne)
             v_more(nv)
 
-        AHEAD = [[(1, 0), (1, 0), (2, 0), (2, 0), (2, 0)], [(0, 2), (1, 1), (1, 1), (2, 0), (2, 0)], [(2, 1), (0, 1), (0, 1), (0, 1), (0, 0)], [(0, 0)] * 5]
-        a_more(3)
-        m_more(2)
-        a_more(5 - 3)
-        r_stats_end(0)
-        r_stats_end(1)
-        t2(0, 1)
-        t2(0, 2)
+        m_more(3)
 
+        AHEAD = [[(2, 0), (2, 0), (2, 0), (2, 0)], [(1, 1), (1, 1), (1, 1), (1, 1)], [(2, 0), (2, 0), (0, 2), (0, 2)], [(0, 0)] * 4]
+        t2(0, 1)
         for u in range(UNITS):
-            last = u == UNITS - 1
             first = u == 0
+            t2(u, 2)
             c2(u, 1)
             a_more(2)
-            if first:
-                t2(0, 0)
-            ahead(u, 0)
+            ahead(*AHEAD[u][0])
             if not first:
                 cy1(u - 1)
+            t2(u, 0)
             c2(u, 2)
             a_more(2)
-            if first:
-                t2(0, 3)
-            else:
+            ahead(*AHEAD[u][1])
+            if not first:
                 cy(u - 1)
                 c_tanh(u - 1)
-            if not last:
-                t2(u + 1, 1)
-            ahead(u, 1)
-            m1(u)
+            t2(u, 3)
             c2(u, 0)
             a_more(2)
+            ahead(*AHEAD[u][2])
+            m1(u)
             if not first:
                 hy(u - 1)
-            ahead(u, 2)
-            if not last:
-                t2(u + 1, 2)
             c2(u, 3)
             a_more(2)
+            ahead(*AHEAD[u][3])
             m2(u)
-            ahead(u, 3)
+            if u + 1 < UNITS:
+                t2(u + 1, 1)
             cp(u)
             c_var(u)
-            if not last:
-                t2(u + 1, 0)
-                ahead(u, 4)
-                t2(u + 1, 3)
         last = UNITS - 1
         cy1(last)
         cy_half(last, 0)

@@ -74,13 +74,13 @@ def tile_multilstm_pa_kernel(
             s1 = small.tile([P, NB], F32, tag="s1")
             st[("s1", u)] = s1
 
+        nc.sync.dma_start(out=h0_sb[:], in_=h0.rearrange("(u p) k -> p u k", p=P))
         load_x()
         for q in range(4):
             load_wih(q)
-        nc.sync.dma_start(out=wi_b[:], in_=lni_w1.partition_broadcast(P))
-        nc.sync.dma_start(out=h0_sb[:], in_=h0.rearrange("(u p) k -> p u k", p=P))
         for n in range(2):
             load_whh(n)
+        nc.sync.dma_start(out=wi_b[:], in_=lni_w1.partition_broadcast(P))
         load_whh(2)
         for u in range(UNITS):
             r_open(u)
@@ -104,7 +104,7 @@ def tile_multilstm_pa_kernel(
         ident_f = const.tile([P, P], F32)
         make_identity(nc, ident_f[:])
 
-        bwide = const.tile([P, GT, P], F32)
+        bcol = const.tile([P, GT], F32)
 
         def prep_bias():
             tpb = ps.tile([P, P], BF16, tag="r", bufs=4)
@@ -115,9 +115,7 @@ def tile_multilstm_pa_kernel(
 
         def spread_bias():
             b2 = st["b2"]
-            bcol = const.tile([P, GT], F32)
             nc.vector.tensor_tensor(out=bcol[:], in0=b2[:, 0:GT], in1=b2[:, GT : 2 * GT], op=ALU.add)
-            nc.vector.tensor_copy(out=bwide[:], in_=bcol[:].unsqueeze(2).to_broadcast([P, GT, P]))
 
         xT_f = const.tile([P, B], F32)
         gram = const.tile([P, V + 1], F32)
@@ -244,11 +242,11 @@ def tile_multilstm_pa_kernel(
         a_banks = {}
 
         def a_matmul(u, n):
-            acc = ps.tile([P, BANK], F32, tag="x", bufs=4)
+            acc = ps.tile([P, BANK], F32, tag="x" if n in (2, 3, 4, 5) else "r", bufs=4)
             for j in range(4):
                 t = 4 * n + j
                 nc.tensor.matmul(
-                    out=acc[:, j * P : (j + 1) * P], lhsT=bwide[:, t, :], rhs=ident_f[:],
+                    out=acc[:, j * P : (j + 1) * P], lhsT=bcol[:, t : t + 1].to_broadcast([P, P]), rhs=ident_f[:],
                     is_transpose=True, start=(j == 0), stop=False,
                 )
             nc.tensor.matmul(
@@ -431,13 +429,10 @@ def tile_multilstm_pa_kernel(
         def words(ap):
             return ap.bitcast(F32)
 
-        WT_AT = {}
+        WT_AT = {2: 0, 3: 1, 4: 2, 5: 3}
+        transpose_rows("h", words(h0_sb[:]), (1, 3))
         x_transposes()
         gram_matrix()
-        a_stats()
-        for q in range(4):
-            prep_wT(q)
-        transpose_rows("h", words(h0_sb[:]), ())
         for n in range(NB + 3):
             if n == 0:
                 quantise("h", h_codes, h_scales)
@@ -447,17 +442,19 @@ def tile_multilstm_pa_kernel(
                 for u in range(2):
                     r_matmul(u, n - 2)
                 for u in range(2):
-                    r_copy(u, n - 2, (n - 2, u) in ())
+                    r_copy(u, n - 2)
+            if n in WT_AT:
+                prep_wT(WT_AT[n])
             if n < NB:
-                transpose_rows(n, words(whh_words[n]), ())
+                transpose_rows(n, words(whh_words[n]), ((0,) if n % 2 else ()))
                 load_more(n + 3)
-            for q in WT_AT.get(n, ()):
-                prep_wT(q)
-            if n == 2:
-                prep_xs()
+            if n == 1:
+                a_stats()
             if n == 4:
-                prep_bias()
+                prep_xs()
             if n == 5:
+                prep_bias()
+            if n == 6:
                 spread_bias()
             if n >= 3:
                 for u in range(2):
@@ -509,7 +506,7 @@ def tile_multilstm_pa_kernel(
 
         AHEAD = [[(2, 0), (2, 0), (2, 0), (2, 0)], [(1, 1), (1, 1), (1, 1), (1, 1)], [(2, 0), (2, 0), (0, 2), (0, 2)], [(0, 0)] * 4]
         t2(0, 1)
-        for u in range(UNITS):
+        for u in range(UNITS - 1):
             first = u == 0
             t2(u, 2)
             c2(u, 1)
@@ -535,12 +532,34 @@ def tile_multilstm_pa_kernel(
             a_more(2)
             ahead(*AHEAD[u][3])
             m2(u)
-            if u + 1 < UNITS:
-                t2(u + 1, 1)
+            t2(u + 1, 1)
+            if u == UNITS - 2:
+                a_more(4)
             cp(u)
             c_var(u)
+        u = UNITS - 1
+        t2(u, 2)
+        c2(u, 1)
+        a_more(2)
+        t2(u, 0)
+        c2(u, 2)
+        a_more(2)
+        m1(u)
+        c2(u, 0)
+        a_more(2)
+        cy1(u - 1)
+
+        m2(u)
+        t2(u, 3)
+        cp(u)
+        c_var(u)
+        cy(u - 1)
+        c_tanh(u - 1)
+        c2(u, 3)
+        cy1(u)
+        hy(u - 1)
+        a_more(2)
         last = UNITS - 1
-        cy1(last)
         cy_half(last, 0)
         cy_half(last, 1)
         hy_half(last, 0)

@@ -64,8 +64,8 @@ def tile_multilstm_pa_kernel(
 
         def load_wih(q):
             nc.sync.dma_start(
-                out=wih_sb[:, 8 * q : 8 * q + 8, 0:V],
-                in_=w_ih1[q * 1024 : (q + 1) * 1024, :].rearrange("(t p) v -> p t v", p=P),
+                out=wih_sb[:, 16 * q : 16 * q + 16, 0:V],
+                in_=w_ih1[q * 2048 : (q + 1) * 2048, :].rearrange("(t p) v -> p t v", p=P),
             )
 
         def r_open(u):
@@ -75,12 +75,13 @@ def tile_multilstm_pa_kernel(
             st[("s1", u)] = s1
 
         nc.sync.dma_start(out=h0_sb[:], in_=h0.rearrange("(u p) k -> p u k", p=P))
+        load_whh(0)
         load_x()
-        for q in range(4):
+        for q in range(2):
             load_wih(q)
-        for n in range(2):
-            load_whh(n)
-        nc.sync.dma_start(out=wi_b[:], in_=lni_w1.partition_broadcast(P))
+        nc.sync.dma_start(out=brow[0:32, :], in_=lni_b1.rearrange("(t p) -> t p", p=P))
+        nc.sync.dma_start(out=brow[32:64, :], in_=lnh_b1.rearrange("(t p) -> t p", p=P))
+        load_whh(1)
         load_whh(2)
         for u in range(UNITS):
             r_open(u)
@@ -88,9 +89,8 @@ def tile_multilstm_pa_kernel(
         def load_more(n):
             if n < NB:
                 load_whh(n)
-            if n == 5:
-                nc.sync.dma_start(out=brow[0:32, :], in_=lni_b1.rearrange("(t p) -> t p", p=P))
-                nc.sync.dma_start(out=brow[32:64, :], in_=lnh_b1.rearrange("(t p) -> t p", p=P))
+            if n == 3:
+                nc.sync.dma_start(out=wi_b[:], in_=lni_w1.partition_broadcast(P))
             if n == NB:
                 nc.sync.dma_start(out=wh_b[:], in_=lnh_w1.partition_broadcast(P))
                 c0_new = hc.tile([P, UNITS, H], BF16, tag="hc")
@@ -104,7 +104,7 @@ def tile_multilstm_pa_kernel(
         ident_f = const.tile([P, P], F32)
         make_identity(nc, ident_f[:])
 
-        bcol = const.tile([P, GT], F32)
+        bwide = const.tile([P, GT, P], F32)
 
         def prep_bias():
             tpb = ps.tile([P, P], BF16, tag="r", bufs=4)
@@ -115,7 +115,9 @@ def tile_multilstm_pa_kernel(
 
         def spread_bias():
             b2 = st["b2"]
+            bcol = const.tile([P, GT], F32)
             nc.vector.tensor_tensor(out=bcol[:], in0=b2[:, 0:GT], in1=b2[:, GT : 2 * GT], op=ALU.add)
+            nc.vector.tensor_copy(out=bwide[:], in_=bcol[:].unsqueeze(2).to_broadcast([P, GT, P]))
 
         xT_f = const.tile([P, B], F32)
         gram = const.tile([P, V + 1], F32)
@@ -246,7 +248,7 @@ def tile_multilstm_pa_kernel(
             for j in range(4):
                 t = 4 * n + j
                 nc.tensor.matmul(
-                    out=acc[:, j * P : (j + 1) * P], lhsT=bcol[:, t : t + 1].to_broadcast([P, P]), rhs=ident_f[:],
+                    out=acc[:, j * P : (j + 1) * P], lhsT=bwide[:, t, :], rhs=ident_f[:],
                     is_transpose=True, start=(j == 0), stop=False,
                 )
             nc.tensor.matmul(
@@ -429,15 +431,15 @@ def tile_multilstm_pa_kernel(
         def words(ap):
             return ap.bitcast(F32)
 
-        WT_AT = {2: 0, 3: 1, 4: 2, 5: 3}
+        WT_AT = {3: 0, 4: 1, 5: 2, 6: 3}
         transpose_rows("h", words(h0_sb[:]), (1, 3))
-        x_transposes()
-        gram_matrix()
         for n in range(NB + 3):
             if n == 0:
                 quantise("h", h_codes, h_scales)
             elif n <= NB:
                 quantise_whh(n - 1)
+            if n == 1:
+                spread_bias()
             if 2 <= n < NB + 2:
                 for u in range(2):
                     r_matmul(u, n - 2)
@@ -446,16 +448,16 @@ def tile_multilstm_pa_kernel(
             if n in WT_AT:
                 prep_wT(WT_AT[n])
             if n < NB:
-                transpose_rows(n, words(whh_words[n]), ((0,) if n % 2 else ()))
+                transpose_rows(n, words(whh_words[n]), ())
                 load_more(n + 3)
+            if n == 0:
+                x_transposes()
+                gram_matrix()
+                prep_bias()
             if n == 1:
                 a_stats()
-            if n == 4:
+            if n == 3:
                 prep_xs()
-            if n == 5:
-                prep_bias()
-            if n == 6:
-                spread_bias()
             if n >= 3:
                 for u in range(2):
                     r_stats(u, n - 3)

@@ -244,7 +244,7 @@ def tile_multilstm_pa_kernel(
         a_banks = {}
 
         def a_matmul(u, n):
-            acc = ps.tile([P, BANK], F32, tag="x" if n in (2, 3, 4, 5) else "r", bufs=4)
+            acc = ps.tile([P, BANK], F32, tag="r" if u == UNITS - 1 and n in (0, 1, 6, 7) else "x", bufs=4)
             for j in range(4):
                 t = 4 * n + j
                 nc.tensor.matmul(
@@ -405,10 +405,10 @@ def tile_multilstm_pa_kernel(
             nc.sync.dma_start(out=out_1[u * P : (u + 1) * P, :], in_=gate(u, 1))
 
         def half(u, k, hh):
-            return r_tiles[u][:, k * H + hh * BANK : k * H + (hh + 1) * BANK]
+            return r_tiles[u][:, k * H + hh * 256 : k * H + (hh + 1) * 256]
 
         def cy_half(u, hh):
-            cols = slice(hh * BANK, (hh + 1) * BANK)
+            cols = slice(hh * 256, (hh + 1) * 256)
             nc.vector.scalar_tensor_tensor(
                 out=half(u, 1, hh), in0=half(u, 2, hh), scalar=st[("crstd", u)][:, 0:1], in1=lwlb[:, 1, cols],
                 op0=ALU.mult, op1=ALU.add,
@@ -417,7 +417,7 @@ def tile_multilstm_pa_kernel(
             nc.scalar.activation(out=half(u, 0, hh), in_=half(u, 1, hh), func=ACT.Tanh)
 
         def hy_half(u, hh):
-            cols = slice(hh * BANK, (hh + 1) * BANK)
+            cols = slice(hh * 256, (hh + 1) * 256)
             nc.vector.tensor_tensor(out=half(u, 3, hh), in0=half(u, 3, hh), in1=half(u, 0, hh), op=ALU.mult)
             nc.sync.dma_start(out=out_0[u * P : (u + 1) * P, cols], in_=half(u, 3, hh))
 
@@ -562,7 +562,7 @@ def tile_multilstm_pa_kernel(
         hy(u - 1)
         a_more(2)
         last = UNITS - 1
-        cy_half(last, 0)
-        cy_half(last, 1)
-        hy_half(last, 0)
-        hy_half(last, 1)
+        for q in range(4):
+            cy_half(last, q)
+        for q in range(4):
+            hy_half(last, q)

@@ -443,8 +443,8 @@ def tile_multilstm_pa_kernel(
             if 2 <= n < NB + 2:
                 for u in range(2):
                     r_matmul(u, n - 2)
-                for u in range(2):
-                    r_copy(u, n - 2)
+                r_copy(0, n - 2)
+                r_evict(1, n - 2, False)
             if n in WT_AT:
                 prep_wT(WT_AT[n])
             if n < NB:
@@ -459,8 +459,7 @@ def tile_multilstm_pa_kernel(
             if n == 3:
                 prep_xs()
             if n >= 3:
-                for u in range(2):
-                    r_stats(u, n - 3)
+                r_stats(0, n - 3)
         ORDER = (2, 3, 4, 5, 0, 1, 6, 7)
         A_SEQ = [(u, n) for u in range(UNITS) for n in ORDER]
         a_next = [0]
@@ -471,8 +470,8 @@ def tile_multilstm_pa_kernel(
             a_next[0] += count
 
         a_more(4)
-        for u in range(2):
-            r_stats_end(u)
+        r_stats_end(0)
+        r_mean(1)
 
         M_SEQ = [(u, n) for u in range(2, UNITS) for n in range(NB)]
         m_next = [0]
@@ -492,7 +491,7 @@ def tile_multilstm_pa_kernel(
                     r_mean(u)
             e_next[0] += count
 
-        V_SEQ = [(u, k) for u in range(2, UNITS) for k in (1, 2, 0, 3)]
+        V_SEQ = [(u, k) for u in range(1, UNITS) for k in (1, 2, 0, 3)]
         v_next = [0]
 
         def v_more(count):
@@ -507,6 +506,7 @@ def tile_multilstm_pa_kernel(
         m_more(3)
 
         AHEAD = [[(2, 0), (2, 0), (2, 0), (2, 0)], [(1, 1), (1, 1), (1, 1), (1, 1)], [(2, 0), (2, 0), (0, 2), (0, 2)], [(0, 0)] * 4]
+        v_more(4)
         t2(0, 1)
         for u in range(UNITS - 1):
             first = u == 0

from contextlib import ExitStack

import concourse.mybir as mybir
from concourse.masks import make_identity

F32 = mybir.dt.float32
BF16 = mybir.dt.bfloat16
U32 = mybir.dt.uint32
U8 = mybir.dt.uint8
FP8X4 = mybir.dt.float8_e4m3fn_x4
ACT = mybir.ActivationFunctionType
ALU = mybir.AluOpType

P = 128
B, V, H = 512, 128, 1024
G = 4 * H
EPS = 1e-5
UNITS = B // P
BANK = 512
NB = G // BANK
GT = G // P
VW = 144
FLOPS = 2 * B * G * (H + V)


def tile_multilstm_pa_kernel(
    tc, x, h0, c0, w_ih1, w_hh1, lni_w1, lni_b1, lnh_w1, lnh_b1, lnc_w1, lnc_b1, out_0, out_1
):
    nc = tc.nc
    with ExitStack() as ctx:
        ctx.enter_context(tc.manual_schedule())
        const = ctx.enter_context(tc.tile_pool(name="const", bufs=1))
        grp_pool = ctx.enter_context(tc.tile_pool(name="grp", bufs=6))
        hc = ctx.enter_context(tc.tile_pool(name="hc", bufs=1))
        land = ctx.enter_context(tc.tile_pool(name="land", bufs=3))
        big = ctx.enter_context(tc.tile_pool(name="big", bufs=4))
        small = ctx.enter_context(tc.tile_pool(name="small", bufs=4))
        ps = ctx.enter_context(tc.psum_pool(name="ps", bufs=4))

        wih_sb = const.tile([P, GT, VW], BF16)
        nc.gpsimd.memset(wih_sb[:, :, V:VW], 1.0)
        brow = const.tile([P, P], BF16)
        nc.vector.memset(brow[64:128, :], 0.0)
        neghalf = const.tile([P, UNITS], F32)
        nc.vector.memset(neghalf[:], -0.5)
        x_sb = const.tile([P, UNITS, V], BF16)
        wi_b = const.tile([P, G], BF16)
        wh_b = const.tile([P, G], BF16)
        h0_sb = hc.tile([P, UNITS, H], BF16, tag="hc")
        lwlb = const.tile([P, 2, H], BF16)
        whh_words = {}
        r_tiles = {}
        st = {}

        def load_whh(n):
            wland = land.tile([P, 4, H], BF16, tag="land")
            whh_words[n] = wland[:]
            nc.sync.dma_start(
                out=wland[:], in_=w_hh1[n * BANK : (n + 1) * BANK, :].rearrange("(t p) k -> p t k", p=P)
            )

        def load_x():
            nc.sync.dma_start(out=x_sb[:], in_=x.rearrange("(u p) v -> p u v", p=P))

        def load_wih(q):
            nc.sync.dma_start(
                out=wih_sb[:, 16 * q : 16 * q + 16, 0:V],
                in_=w_ih1[q * 2048 : (q + 1) * 2048, :].rearrange("(t p) v -> p t v", p=P),
            )

        def r_open(u):
            r_new = big.tile([P, G], F32, tag="big")
            r_tiles[u] = r_new
            s1 = small.tile([P, NB], F32, tag="s1")
            st[("s1", u)] = s1

        nc.sync.dma_start(out=h0_sb[:], in_=h0.rearrange("(u p) k -> p u k", p=P))
        load_whh(0)
        load_x()
        for q in range(2):
            load_wih(q)
        nc.sync.dma_start(out=brow[0:32, :], in_=lni_b1.rearrange("(t p) -> t p", p=P))
        nc.sync.dma_start(out=brow[32:64, :], in_=lnh_b1.rearrange("(t p) -> t p", p=P))
        load_whh(1)
        load_whh(2)
        for u in range(UNITS):
            r_open(u)

        def load_more(n):
            if n < NB:
                load_whh(n)
            if n == 3:
                nc.sync.dma_start(out=wi_b[:], in_=lni_w1.partition_broadcast(P))
            if n == NB:
                nc.sync.dma_start(out=wh_b[:], in_=lnh_w1.partition_broadcast(P))
                c0_new = hc.tile([P, UNITS, H], BF16, tag="hc")
                st["c0"] = c0_new
                nc.sync.dma_start(out=c0_new[:], in_=c0.rearrange("(u p) k -> p u k", p=P))
                nc.sync.dma_start(out=lwlb[:, 0, :], in_=lnc_w1.partition_broadcast(P))
                nc.sync.dma_start(out=lwlb[:, 1, :], in_=lnc_b1.partition_broadcast(P))

        ident_b = const.tile([P, P], BF16)
        make_identity(nc, ident_b[:])
        ident_f = const.tile([P, P], F32)
        make_identity(nc, ident_f[:])

        bwide = const.tile([P, GT, P], F32)

        def prep_bias():
            tpb = ps.tile([P, P], BF16, tag="r", bufs=4)
            nc.tensor.transpose(tpb[:], brow[:], ident_b[:])
            b2 = const.tile([P, 2 * GT], F32)
            nc.scalar.copy(out=b2[:], in_=tpb[:, 0 : 2 * GT])
            st["b2"] = b2

        def spread_bias():
            b2 = st["b2"]
            bcol = const.tile([P, GT], F32)
            nc.vector.tensor_tensor(out=bcol[:], in0=b2[:, 0:GT], in1=b2[:, GT : 2 * GT], op=ALU.add)
            nc.vector.tensor_copy(out=bwide[:], in_=bcol[:].unsqueeze(2).to_broadcast([P, GT, P]))

        xT_f = const.tile([P, B], F32)
        gram = const.tile([P, V + 1], F32)
        wneg = const.tile([P, 1], F32)
        rstd4 = const.tile([P, UNITS], F32)

        def x_transposes():
            tpx = ps.tile([P, UNITS, P], BF16, tag="r", bufs=4)
            for u in range(UNITS):
                nc.tensor.transpose(tpx[:, u, :], x_sb[:, u, :], ident_b[:])
            nc.scalar.copy(out=xT_f[:], in_=tpx[:].rearrange("p u b -> p (u b)"))

        def gram_matrix():
            gram_ps = ps.tile([P, V + 1], F32, tag="r", bufs=4)
            for t in range(GT):
                nc.tensor.matmul(
                    out=gram_ps[:], lhsT=wih_sb[:, t, 0:V], rhs=wih_sb[:, t, 0 : V + 1],
                    start=(t == 0), stop=(t == GT - 1),
                )
            nc.scalar.copy(out=gram[:], in_=gram_ps[:])
            nc.scalar.activation(out=wneg[:], in_=gram[:, V : V + 1], func=ACT.Identity, scale=-1.0 / G)

        def a_stats():
            q4 = const.tile([P, UNITS], F32)
            mean4 = const.tile([P, UNITS], F32)
            y_ps = {}
            for g in range(2):
                y_new = ps.tile([P, 2, 256], F32, tag="r", bufs=4)
                for i in range(2):
                    u = 2 * g + i
                    nc.tensor.matmul(
                        out=y_new[:, i, 0 : V + 1], lhsT=xT_f[:, u * P : (u + 1) * P], rhs=gram[:], start=True, stop=True
                    )
                    y_ps[u] = y_new[:, i, :]
            for u in range(UNITS):
                yjunk = small.tile([P, V], F32, tag="yjunk")
                nc.vector.scalar_tensor_tensor(
                    out=yjunk[:], in0=y_ps[u][:, 0:V], scalar=1.0 / G, in1=x_sb[:, u, :], op0=ALU.mult, op1=ALU.mult,
                    accum_out=q4[:, u : u + 1],
                )
                nc.vector.tensor_scalar(
                    out=mean4[:, u : u + 1], in0=y_ps[u][:, V : V + 1], scalar1=1.0 / G, scalar2=None, op0=ALU.mult
                )
            msq4 = const.tile([P, UNITS], F32)
            nc.vector.tensor_tensor(out=msq4[:], in0=mean4[:], in1=mean4[:], op=ALU.mult)
            var4 = const.tile([P, UNITS], F32)
            nc.vector.tensor_tensor(out=var4[:], in0=q4[:], in1=msq4[:], op=ALU.subtract)
            veps4 = const.tile([P, UNITS], F32)
            nc.gpsimd.tensor_scalar(out=veps4[:], in0=var4[:], scalar1=0.0, scalar2=EPS, op0=ALU.max, op1=ALU.add)
            nc.gpsimd.tensor_tensor(out=rstd4[:], in0=veps4[:], in1=neghalf[:], op=ALU.pow)

        h_codes = const.tile([P, 2, B], U32, align_bytes=64)
        h_scales = const.tile([P, 2, B], U8, align_bytes=64)
        w_codes = const.tile([P, 2, G], U32, align_bytes=64)
        w_scales = const.tile([P, 2, G], U8, align_bytes=64)
        wT = const.tile([P, G], F32)
        xs = const.tile([P, UNITS, V], F32)
        xsT = const.tile([P, B], F32)
        grp_tiles = {}

        perm_tiles = {}

        def even_odd(key, src_words, engine):
            new = hc.tile([P, 4, 2, 2, P], F32, tag="perm")
            dst = new[:].rearrange("p r c s w -> p (r c) s w")
            src = src_words.rearrange("p r (c w s) -> p (r c) s w", c=2, s=2)
            if engine == "v":
                nc.vector.tensor_copy(out=dst, in_=src)
            else:
                nc.scalar.copy(out=dst, in_=src)
            perm_tiles[key] = new

        def transpose_rows(key, src_words, on_vector):
            for c in range(2):
                grp = grp_pool.tile([P, 4 * BANK], BF16, tag="grp", align_bytes=64)
                grpw = grp[:].bitcast(F32).rearrange("p (r s) -> p r s", s=2)
                for half in range(2):
                    tp = ps.tile([P, 2, 256], F32, tag="x", bufs=4)
                    for s in range(2):
                        for j in range(2):
                            if key in perm_tiles:
                                piece = perm_tiles[key][:, 2 * half + j, c, s, :]
                            else:
                                piece = src_words[:, 2 * half + j, 256 * c + s : 256 * (c + 1) : 2]
                            nc.tensor.transpose(tp[:, s, j * P : (j + 1) * P], piece, ident_f[:])
                    dst = grpw[:, half * 256 : (half + 1) * 256, :]
                    src = tp[:].rearrange("p s r -> p r s")
                    if 2 * c + half in on_vector:
                        nc.vector.tensor_copy(out=dst, in_=src)
                    else:
                        nc.scalar.copy(out=dst, in_=src)
                grp_tiles[(key, c)] = grp

        def quantise(key, codes, scales):
            for c in range(2):
                nc.vector.quantize_mx(
                    out=codes[:, c, :].bitcast(FP8X4), scales=scales[:, c, :], in_=grp_tiles[(key, c)][:]
                )

        def quantise_whh(n):
            cols = slice(n * BANK, (n + 1) * BANK)
            quantise(n, w_codes[:, :, cols], w_scales[:, :, cols])

        def prep_wT(q):
            tpw = ps.tile([P, 8, P], BF16, tag="r", bufs=4)
            for j in range(8):
                nc.tensor.transpose(tpw[:, j, :], wih_sb[:, 8 * q + j, 0:V], ident_b[:])
            cols = slice(q * 1024, (q + 1) * 1024)
            nc.vector.scalar_tensor_tensor(
                out=wT[:, cols], in0=tpw[:].rearrange("p j g -> p (j g)"), scalar=wneg[:, 0:1], in1=wi_b[:, cols],
                op0=ALU.add, op1=ALU.mult,
            )

        def prep_xs():
            for u in range(UNITS):
                nc.vector.tensor_scalar(
                    out=xs[:, u, :], in0=x_sb[:, u, :], scalar1=rstd4[:, u : u + 1], scalar2=None, op0=ALU.mult
                )
            tps = ps.tile([P, UNITS, P], F32, tag="r", bufs=4)
            for u in range(UNITS):
                nc.tensor.transpose(tps[:, u, :], xs[:, u, :], ident_f[:])
            nc.scalar.copy(out=xsT[:], in_=tps[:].rearrange("p u b -> p (u b)"))

        a_banks = {}

        def a_matmul(u, n):
            acc = ps.tile([P, BANK], F32, tag="r" if u == UNITS - 1 and n in (0, 1, 6, 7) else "x", bufs=4)
            for j in range(4):
                t = 4 * n + j
                nc.tensor.matmul(
                    out=acc[:, j * P : (j + 1) * P], lhsT=bwide[:, t, :], rhs=ident_f[:],
                    is_transpose=True, start=(j == 0), stop=False,
                )
            nc.tensor.matmul(
                out=acc[:], lhsT=xsT[:, u * P : (u + 1) * P], rhs=wT[:, n * BANK : (n + 1) * BANK],
                start=False, stop=True,
            )
            a_banks[(u, n)] = acc

        r_banks = {}

        def r_matmul(u, n):
            rows = slice(u * P, (u + 1) * P)
            cols = slice(n * BANK, (n + 1) * BANK)
            acc = ps.tile([P, BANK], F32, tag="r", bufs=4)
            for c in range(2):
                nc.tensor.matmul_mx(
                    out=acc[:],
                    lhsT=h_codes[:, c, rows].bitcast(FP8X4),
                    lhsT_scale=h_scales[:, c, rows],
                    rhs=w_codes[:, c, cols].bitcast(FP8X4),
                    rhs_scale=w_scales[:, c, cols],
                    start=(c == 0),
                    stop=(c == 1),
                )
            r_banks[(u, n)] = acc

        def r_evict(u, n, on_vector=False):
            cols = slice(n * BANK, (n + 1) * BANK)
            s1 = st[("s1", u)][:, n : n + 1]
            if on_vector:
                nc.vector.tensor_scalar(
                    out=r_tiles[u][:, cols], in0=r_banks[(u, n)][:], scalar1=1.0, scalar2=None, op0=ALU.mult, op1=ALU.add,
                    accum_out=s1,
                )
                return
            nc.scalar.activation(out=r_tiles[u][:, cols], in_=r_banks[(u, n)][:], func=ACT.Identity, accum_out=s1)

        def r_copy(u, n, on_vector=False):
            cols = slice(n * BANK, (n + 1) * BANK)
            if on_vector:
                nc.vector.tensor_copy(out=r_tiles[u][:, cols], in_=r_banks[(u, n)][:])
            else:
                nc.scalar.copy(out=r_tiles[u][:, cols], in_=r_banks[(u, n)][:])

        def r_stats(u, n):
            if n == 0:
                bst = small.tile([P, NB, 6], F32, tag="bst")
                st[("bst", u)] = bst
            nc.vector.bn_stats(out=st[("bst", u)][:, n, :], in_=r_tiles[u][:, n * BANK : (n + 1) * BANK])

        def r_stats_end(u):
            mv = small.tile([P, 2], F32, tag="mv")
            nc.vector.bn_aggr(out=mv[:], in_=st[("bst", u)][:].rearrange("p n s -> p (n s)"))
            veps = small.tile([P, 1], F32, tag="veps")
            nc.gpsimd.tensor_scalar(out=veps[:], in0=mv[:, 1:2], scalar1=0.0, scalar2=EPS, op0=ALU.max, op1=ALU.add)
            rstd = small.tile([P, 1], F32, tag="rstd")
            nc.gpsimd.tensor_tensor(out=rstd[:], in0=veps[:], in1=neghalf[:, 0:1], op=ALU.pow)
            st[("mean", u)] = mv
            st[("rstd", u)] = rstd

        def r_mean(u):
            s1junk = small.tile([P, NB], F32, tag="s1junk")
            negmean = small.tile([P, 1], F32, tag="negmean")
            nc.scalar.activation(
                out=s1junk[:], in_=st[("s1", u)][:], func=ACT.Identity, scale=-1.0 / G, accum_out=negmean[:]
            )
            ssq = small.tile([P, 4], F32, tag="ssq")
            st[("negmean", u)] = negmean
            st[("ssq", u)] = ssq

        def r_var(u, k):
            junk = grp_pool.tile([P, 2048], BF16, tag="grp", align_bytes=64)
            nc.scalar.activation(
                out=junk[:, 0:H], in_=r_tiles[u][:, k * H : (k + 1) * H], func=ACT.Square,
                bias=st[("negmean", u)][:, 0:1], scale=1.0, accum_out=st[("ssq", u)][:, k : k + 1],
            )
            st[("nvar", u)] = st.get(("nvar", u), 0) + 1
            if st[("nvar", u)] == 4:
                ssq = st[("ssq", u)]
                vjunk = small.tile([P, 4], F32, tag="vjunk")
                veps = small.tile([P, 1], F32, tag="veps")
                nc.scalar.activation(
                    out=vjunk[:], in_=ssq[:], func=ACT.Identity, bias=EPS / 4.0, scale=1.0 / G, accum_out=veps[:]
                )
                rstd = small.tile([P, 1], F32, tag="rstd")
                nc.gpsimd.tensor_tensor(out=rstd[:], in0=veps[:], in1=neghalf[:, 0:1], op=ALU.pow)
                st[("rstd", u)] = rstd

        def t2(u, k):
            cols = slice(k * H, (k + 1) * H)
            if ("mean", u) in st:
                centre, op = st[("mean", u)], ALU.subtract
            else:
                centre, op = st[("negmean", u)], ALU.add
            nc.vector.scalar_tensor_tensor(
                out=r_tiles[u][:, cols], in0=r_tiles[u][:, cols], scalar=centre[:, 0:1],
                in1=wh_b[:, cols], op0=op, op1=ALU.mult,
            )

        funcs = [ACT.Sigmoid, ACT.Sigmoid, ACT.Tanh, ACT.Sigmoid]

        def c2(u, k):
            for n in (2 * k, 2 * k + 1):
                cols = slice(n * BANK, (n + 1) * BANK)
                nc.vector.scalar_tensor_tensor(
                    out=r_tiles[u][:, cols], in0=r_tiles[u][:, cols], scalar=st[("rstd", u)][:, 0:1],
                    in1=a_banks[(u, n)][:], op0=ALU.mult, op1=ALU.add,
                )
            nc.scalar.activation(out=gate(u, k), in_=gate(u, k), func=funcs[k])

        def gate(u, k):
            return r_tiles[u][:, k * H : (k + 1) * H]

        def m1(u):
            nc.vector.tensor_tensor(out=gate(u, 1), in0=gate(u, 1), in1=st["c0"][:, u, :], op=ALU.mult)

        def m2(u):
            nc.vector.tensor_tensor(out=gate(u, 0), in0=gate(u, 0), in1=gate(u, 2), op=ALU.mult)

        def cp(u):
            csum = small.tile([P, 1], F32, tag="csum")
            nc.vector.scalar_tensor_tensor(
                out=gate(u, 0), in0=gate(u, 0), scalar=1.0, in1=gate(u, 1), op0=ALU.mult, op1=ALU.add,
                accum_out=csum[:],
            )
            cneg = small.tile([P, 1], F32, tag="cneg")
            nc.scalar.activation(out=cneg[:], in_=csum[:], func=ACT.Identity, scale=-1.0 / H)
            st[("cneg", u)] = cneg

        def c_var(u):
            cssq = small.tile([P, 1], F32, tag="cssq")
            cjunk = grp_pool.tile([P, 2048], BF16, tag="grp", align_bytes=64)
            nc.scalar.activation(
                out=cjunk[:, 0:H], in_=gate(u, 0), func=ACT.Square, bias=st[("cneg", u)][:, 0:1], scale=1.0,
                accum_out=cssq[:],
            )
            cveps = small.tile([P, 1], F32, tag="cveps")
            nc.scalar.activation(out=cveps[:], in_=cssq[:], func=ACT.Identity, bias=EPS, scale=1.0 / H)
            crstd = small.tile([P, 1], F32, tag="crstd")
            nc.gpsimd.tensor_tensor(out=crstd[:], in0=cveps[:], in1=neghalf[:, 0:1], op=ALU.pow)
            st[("crstd", u)] = crstd

        def cy1(u):
            nc.vector.scalar_tensor_tensor(
                out=gate(u, 2), in0=gate(u, 0), scalar=st[("cneg", u)][:, 0:1], in1=lwlb[:, 0, :],
                op0=ALU.add, op1=ALU.mult,
            )

        def cy(u):
            nc.vector.scalar_tensor_tensor(
                out=gate(u, 1), in0=gate(u, 2), scalar=st[("crstd", u)][:, 0:1], in1=lwlb[:, 1, :],
                op0=ALU.mult, op1=ALU.add,
            )
            nc.sync.dma_start(out=out_1[u * P : (u + 1) * P, :], in_=gate(u, 1))

        def half(u, k, hh):
            return r_tiles[u][:, k * H + hh * 256 : k * H + (hh + 1) * 256]

        def cy_half(u, hh):
            cols = slice(hh * 256, (hh + 1) * 256)
            nc.vector.scalar_tensor_tensor(
                out=half(u, 1, hh), in0=half(u, 2, hh), scalar=st[("crstd", u)][:, 0:1], in1=lwlb[:, 1, cols],
                op0=ALU.mult, op1=ALU.add,
            )
            nc.sync.dma_start(out=out_1[u * P : (u + 1) * P, cols], in_=half(u, 1, hh))
            nc.scalar.activation(out=half(u, 0, hh), in_=half(u, 1, hh), func=ACT.Tanh)

        def hy_half(u, hh):
            cols = slice(hh * 256, (hh + 1) * 256)
            nc.vector.tensor_tensor(out=half(u, 3, hh), in0=half(u, 3, hh), in1=half(u, 0, hh), op=ALU.mult)
            nc.sync.dma_start(out=out_0[u * P : (u + 1) * P, cols], in_=half(u, 3, hh))

        def c_tanh(u):
            nc.scalar.activation(out=gate(u, 0), in_=gate(u, 1), func=ACT.Tanh)

        def hy(u):
            nc.vector.tensor_tensor(out=gate(u, 3), in0=gate(u, 3), in1=gate(u, 0), op=ALU.mult)
            nc.sync.dma_start(out=out_0[u * P : (u + 1) * P, :], in_=gate(u, 3))

        def words(ap):
            return ap.bitcast(F32)

        WT_AT = {3: 0, 4: 1, 5: 2, 6: 3}
        transpose_rows("h", words(h0_sb[:]), (1, 3))
        for n in range(NB + 3):
            if n == 0:
                quantise("h", h_codes, h_scales)
            elif n <= NB:
                quantise_whh(n - 1)
            if n == 1:
                spread_bias()
            if 2 <= n < NB + 2:
                for u in range(2):
                    r_matmul(u, n - 2)
                r_copy(0, n - 2)
                r_evict(1, n - 2, False)
            if n in WT_AT:
                prep_wT(WT_AT[n])
            if n < NB:
                transpose_rows(n, words(whh_words[n]), ())
                load_more(n + 3)
            if n == 0:
                x_transposes()
                gram_matrix()
                prep_bias()
            if n == 1:
                a_stats()
            if n == 3:
                prep_xs()
            if n >= 3:
                r_stats(0, n - 3)
        ORDER = (2, 3, 4, 5, 0, 1, 6, 7)
        A_SEQ = [(u, n) for u in range(UNITS) for n in ORDER]
        a_next = [0]

        def a_more(count):
            for u, n in A_SEQ[a_next[0] : a_next[0] + count]:
                a_matmul(u, n)
            a_next[0] += count

        a_more(4)
        r_stats_end(0)
        r_mean(1)

        M_SEQ = [(u, n) for u in range(2, UNITS) for n in range(NB)]
        m_next = [0]

        def m_more(count):
            for u, n in M_SEQ[m_next[0] : m_next[0] + count]:
                r_matmul(u, n)
            m_next[0] += count

        e_next = [0]

        def e_more(count):
            for u, n in M_SEQ[e_next[0] : e_next[0] + count]:
                r_evict(u, n)
                m_more(1)
                if n == NB - 1:
                    r_mean(u)
            e_next[0] += count

        V_SEQ = [(u, k) for u in range(1, UNITS) for k in (1, 2, 0, 3)]
        v_next = [0]

        def v_more(count):
            for u, k in V_SEQ[v_next[0] : v_next[0] + count]:
                r_var(u, k)
            v_next[0] += count

        def ahead(ne, nv):
            e_more(ne)
            v_more(nv)

        m_more(3)

        AHEAD = [[(2, 0), (2, 0), (2, 0), (2, 0)], [(1, 1), (1, 1), (1, 1), (1, 1)], [(2, 0), (2, 0), (0, 2), (0, 2)], [(0, 0)] * 4]
        v_more(4)
        t2(0, 1)
        for u in range(UNITS - 1):
            first = u == 0
            t2(u, 2)
            c2(u, 1)
            a_more(2)
            ahead(*AHEAD[u][0])
            if not first:
                cy1(u - 1)
            t2(u, 0)
            c2(u, 2)
            a_more(2)
            ahead(*AHEAD[u][1])
            if not first:
                cy(u - 1)
                c_tanh(u - 1)
            t2(u, 3)
            c2(u, 0)
            a_more(2)
            ahead(*AHEAD[u][2])
            m1(u)
            if not first:
                hy(u - 1)
            c2(u, 3)
            a_more(2)
            ahead(*AHEAD[u][3])
            m2(u)
            t2(u + 1, 1)
            if u == UNITS - 2:
                a_more(4)
            cp(u)
            c_var(u)
        u = UNITS - 1
        t2(u, 2)
        c2(u, 1)
        a_more(2)
        t2(u, 0)
        c2(u, 2)
        a_more(2)
        m1(u)
        c2(u, 0)
        a_more(2)
        cy1(u - 1)

        m2(u)
        t2(u, 3)
        cp(u)
        c_var(u)
        cy(u - 1)
        c_tanh(u - 1)
        c2(u, 3)
        cy1(u)
        hy(u - 1)
        a_more(2)
        last = UNITS - 1
        for q in range(4):
            cy_half(last, q)
        for q in range(4):
            hy_half(last, q)
